import numpy as np
import ml_dtypes


def mxq(x, axis, fmt="e4m3"):
    dtype, down = {"e4m3": (ml_dtypes.float8_e4m3fn, 7), "e5m2": (ml_dtypes.float8_e5m2, 14)}[fmt]
    v = np.moveaxis(np.asarray(x, np.float32).astype(ml_dtypes.bfloat16).astype(np.float64), axis, -1)
    blocks = v.reshape(v.shape[:-1] + (-1, 32))
    amax = np.abs(blocks).max(-1, keepdims=True)
    byte = np.maximum(np.where(amax > 0, np.frexp(amax)[1] - 1 + 127, 0) - down, 1)
    scale = np.exp2(byte - 127.0)
    codes = (blocks / scale).astype(np.float32).astype(dtype).astype(np.float64)
    return np.moveaxis((codes * scale).reshape(v.shape), -1, axis)


WIDE = False


def mx_kscale(k):
    if not WIDE:
        return np.ones(k)
    levels = np.array([10, -10, 5, -5, 0])
    a = np.random.permutation(np.resize(levels, k // 512 * 4)).reshape(k // 512, 4)
    idx = np.arange(k)
    return np.exp2(a[idx // 512, idx % 128 // 32])


BF16 = ml_dtypes.bfloat16


def bf(x):
    return np.asarray(x, np.float32).astype(BF16)


def f64(x):
    return np.asarray(x).astype(np.float64)


B, L, V, N = 2, 2048, 1024, 512


def _sanitize(x):
    return np.nan_to_num(x, nan=0.0, posinf=1e4, neginf=-1e4)


def _safe_acosh(x):
    xm1 = np.maximum(x - 1.0, 0.0)
    near = xm1 < 1e-3
    taylor = np.sqrt(2.0 * np.maximum(xm1, 1e-12)) * (1.0 - xm1 / 12.0)
    exact = np.arccosh(np.maximum(x, 1.0 + 1e-7))
    return np.where(near, taylor, exact)


def setup_inputs():
    s = mx_kscale(N)
    c = np.exp2(np.round(0.5 * np.log2(np.mean(1.0 / (s * s)))))
    m = np.random.standard_normal(N)
    sp = (np.random.standard_normal((B, L, N)) + np.random.uniform(-1.5, 1.5, (B, L, 1)) * m) / np.sqrt(N)
    t = np.sqrt(1.0 + np.sum(sp * sp, axis=-1, keepdims=True))
    w = (np.random.standard_normal((V, N)) + np.random.uniform(-1.5, 1.5, (V, 1)) * m) * 0.7 / np.sqrt(N)
    return {"hidden_states": bf(np.concatenate([t, sp * (s * c)], axis=-1)), "weight": bf(w / (s * c)),
            "logit_scale": bf(0.6 + 0.1 * np.random.standard_normal(1))}


def reference(hidden_states, weight, logit_scale):
    h = _sanitize(f64(hidden_states))
    weight = f64(weight)
    norm = np.linalg.norm(weight, axis=-1)
    r = np.where(norm > 1e-7, np.sinh(norm) / np.maximum(norm, 1e-7), 1.0)
    w_time = np.cosh(norm)
    w_space = r[:, None] * weight
    dot = mxq(h[..., 1:], 2, "e4m3") @ mxq(w_space, 1, "e4m3").T
    x = h[..., :1] * w_time[None, None, :] - dot
    d = _safe_acosh(x)
    tau = np.clip(f64(logit_scale), 0.01, 2.5)
    logits = -tau * d * d
    return _sanitize(logits)

@@ -1,0 +1,392 @@
+from contextlib import ExitStack
+
+import concourse.mybir as mybir
+from concourse.masks import make_identity
+
+F32 = mybir.dt.float32
+BF16 = mybir.dt.bfloat16
+U32 = mybir.dt.uint32
+U8 = mybir.dt.uint8
+FP8X4 = mybir.dt.float8_e4m3fn_x4
+ALU = mybir.AluOpType
+ACT = mybir.ActivationFunctionType
+
+P = 128
+NTOK = 4096
+V = 1024
+K = 512
+HB = 512
+NT = NTOK // P
+SLOT = 528
+FMAX = 3.3896e38
+FLOPS = 2 * NTOK * V * K
+C_ON_G = False
+BATCHES = [10,10]
+LA = 3
+W1AT = 3
+PREP_FROM = 4
+PREP_EVERY = 2
+TS_LATE_AT = 5
+
+
+def make_units():
+    units = [[(0, 0)], [(1, 0)], [(2, 0), (3, 0)]]
+    units.append([(i, 0) for i in range(4, 8)])
+    units.append([(i, 1) for i in range(0, 4)])
+    units.append([(i, 1) for i in range(4, 8)])
+    for i in range(8, 30, 2):
+        units.append([(i, 0), (i, 1), (i + 1, 0), (i + 1, 1)])
+    units.extend([[(30, 0), (30, 1)], [(31, 0)], [(31, 1)]])
+    return units
+
+
+def tile_geodesiclmheadv2_t_kernel(tc, hidden_states, weight, logit_scale, out):
+    nc = tc.nc
+    hid = hidden_states.flatten_outer_dims().rearrange("(p i) c -> p i c", i=NT)
+    out3 = out.flatten_outer_dims().rearrange("(p i) v -> p i v", i=NT)
+    outv = out.flatten_outer_dims().rearrange("(p i) v -> p (i v)", i=NT)
+    wv = weight.rearrange("(j p) k -> p j k", p=P)
+    units = make_units()
+
+    with ExitStack() as ctx:
+        const = ctx.enter_context(tc.tile_pool(name="const", bufs=1))
+        hgp = ctx.enter_context(tc.tile_pool(name="hgp", bufs=4))
+        xp = ctx.enter_context(tc.tile_pool(name="xp", bufs=4))
+        app = ctx.enter_context(tc.tile_pool(name="app", bufs=10))
+        tpp = ctx.enter_context(tc.psum_pool(name="tpp", bufs=4))
+        accp = ctx.enter_context(tc.psum_pool(name="accp", bufs=4))
+        ctx.enter_context(tc.manual_schedule())
+
+        ident = const.tile([P, P], F32, name="ident")
+        one = const.tile([P, 1], F32, name="one")
+        warm = const.tile([P, 1], F32, name="warm")
+        make_identity(nc, ident[:])
+        nc.vector.memset(one[:], 1.0)
+        nc.scalar.activation(out=warm[:], in_=one[:], func=ACT.Sqrt)
+
+        wraw = [const.tile([P, 2 * K], BF16, name="wraw%d" % a) for a in range(4)]
+        for a in range(4):
+            nc.sync.dma_start(
+                out=wraw[a][:].rearrange("p (j k) -> p j k", k=K), in_=wv[:, 2 * a : 2 * a + 2, :]
+            )
+        hraw = [const.tile([P, 8 * SLOT], BF16, name="hraw%d" % c) for c in range(4)]
+        ls = const.tile([P, 1], BF16, name="ls")
+        for c in range(4):
+            nc.sync.dma_start(
+                out=hraw[c][:].rearrange("p (i c) -> p i c", c=SLOT)[:, :, 1 : K + 2],
+                in_=hid[:, 8 * c : 8 * c + 8, :],
+            )
+            if c == 0:
+                nc.sync.dma_start(out=ls[:], in_=logit_scale.partition_broadcast(P))
+
+        traw = const.tile([P, NT], F32, name="traw")
+        tfin = const.tile([P, NT], F32, name="tfin")
+        tcl = const.tile([P, NT], F32, name="tcl")
+        tkp = const.tile([P, NT], F32, name="tkp")
+        tkn = const.tile([P, NT], F32, name="tkn")
+        ts = const.tile([P, NT], F32, name="ts")
+
+        def time_coordinate(c0, c1):
+            for c in range(c0, c1):
+                nc.gpsimd.tensor_copy(
+                    out=traw[:, 8 * c : 8 * c + 8].unsqueeze(2),
+                    in_=hraw[c][:].rearrange("p (i c) -> p i c", c=SLOT)[:, :, 1:2],
+                )
+            s = slice(8 * c0, 8 * c1)
+            nc.gpsimd.tensor_scalar(out=tfin[:, s], in0=traw[:, s], scalar1=0.0, scalar2=0.0, op0=ALU.mult, op1=ALU.is_equal)
+            nc.gpsimd.tensor_scalar(out=tcl[:, s], in0=traw[:, s], scalar1=-FMAX, scalar2=FMAX, op0=ALU.max, op1=ALU.min)
+            nc.gpsimd.tensor_tensor(out=tcl[:, s], in0=tcl[:, s], in1=tfin[:, s], op=ALU.mult)
+            nc.gpsimd.tensor_scalar(out=tkp[:, s], in0=traw[:, s], scalar1=FMAX, scalar2=1.0e4, op0=ALU.is_gt, op1=ALU.mult)
+            nc.gpsimd.tensor_scalar(out=tkn[:, s], in0=traw[:, s], scalar1=-FMAX, scalar2=-1.0e4, op0=ALU.is_lt, op1=ALU.mult)
+            nc.gpsimd.tensor_tensor(out=tkp[:, s], in0=tkp[:, s], in1=tkn[:, s], op=ALU.add)
+            nc.gpsimd.tensor_tensor(out=ts[:, s], in0=tcl[:, s], in1=tkp[:, s], op=ALU.add)
+
+        time_coordinate(0, 1)
+        tau = const.tile([P, 1], F32, name="tau")
+        m4tau = const.tile([P, 1], F32, name="m4tau")
+        nc.gpsimd.tensor_scalar(out=tau[:], in0=ls[:], scalar1=0.01, scalar2=2.5, op0=ALU.max, op1=ALU.min)
+        nc.gpsimd.tensor_scalar(out=m4tau[:], in0=tau[:], scalar1=-4.0, scalar2=0.0, op0=ALU.mult, op1=ALU.add)
+
+        hc = [const.tile([P, 4 * P], U32, name="hc%d" % g, align_bytes=64) for g in range(8)]
+        hs = [const.tile([P, 4 * P], U8, name="hs%d" % g, align_bytes=64) for g in range(8)]
+        hg_of = {}
+        tph_of = {}
+
+        def h_transpose(g):
+            for half in range(2):
+                tph = tpp.tile([P, HB], F32, name="tph", tag="tp")
+                tph_of[(g, half)] = tph
+                for ii in range(2):
+                    i = 4 * g + 2 * half + ii
+                    h32 = hraw[i // 8][:].bitcast(F32)
+                    base = (i % 8) * (SLOT // 2) + 1
+                    for u in range(2):
+                        nc.tensor.transpose(
+                            out=tph[:, u * 256 + ii * P : u * 256 + (ii + 1) * P],
+                            in_=h32[:, base + u * P : base + (u + 1) * P],
+                            identity=ident[:],
+                        )
+
+        def h_evac(g, half, eng):
+            if half == 0:
+                hg_of[g] = hgp.tile([P, 16 * P], BF16, name="hg", tag="hg", align_bytes=64)
+            hg32 = hg_of[g][:].bitcast(F32).rearrange("p (t u) -> p t u", u=2)
+            dst = hg32[:, half * 256 : (half + 1) * 256, :]
+            src = tph_of[(g, half)][:].rearrange("p (u t) -> p t u", u=2)
+            if eng == "v":
+                nc.vector.tensor_copy(out=dst, in_=src)
+            else:
+                nc.scalar.copy(out=dst, in_=src)
+
+        def h_quantise(g):
+            nc.vector.quantize_mx(out=hc[g][:].bitcast(FP8X4), scales=hs[g][:], in_=hg_of[g][:])
+
+        n2s = const.tile([P, 8], F32, name="n2s")
+        n2 = const.tile([P, 8], F32, name="n2")
+        junk = const.tile([P, K], BF16, name="junk")
+        sqv = const.tile([P, K], F32, name="sqv")
+
+        def wrow(j):
+            return wraw[j // 2][:, (j % 2) * K : (j % 2 + 1) * K]
+
+        for j in (0, 1, 4, 5):
+            nc.scalar.activation(out=junk[:], in_=wrow(j), func=ACT.Square, accum_out=n2s[:, j : j + 1])
+        for j in (2, 3, 6, 7):
+            nc.vector.scalar_tensor_tensor(
+                out=sqv[:], in0=wrow(j), scalar=1.0, in1=wrow(j), op0=ALU.mult, op1=ALU.mult,
+                accum_out=n2[:, j : j + 1],
+            )
+        nc.vector.tensor_copy(
+            out=n2[:].rearrange("p (a b) -> p a b", b=4)[:, :, 0:2],
+            in_=n2s[:].rearrange("p (a b) -> p a b", b=4)[:, :, 0:2],
+        )
+        nc.vector.tensor_scalar_max(out=n2[:], in0=n2[:], scalar1=1.0e-30)
+
+        nrm = const.tile([P, 8], F32, name="nrm")
+        ep = const.tile([P, 8], F32, name="ep")
+        em = const.tile([P, 8], F32, name="em")
+        nc.scalar.activation(out=nrm[:], in_=n2[:], func=ACT.Sqrt)
+        nc.scalar.activation(out=ep[:], in_=nrm[:], func=ACT.Exp)
+        nc.scalar.activation(out=em[:], in_=nrm[:], func=ACT.Exp, scale=-1.0)
+
+        nm = const.tile([P, 8], F32, name="nm")
+        rn = const.tile([P, 8], F32, name="rn")
+        big = const.tile([P, 8], F32, name="big")
+        c1 = const.tile([P, 8], F32, name="c1")
+        c0 = const.tile([P, 8], F32, name="c0")
+        sh = const.tile([P, 8], F32, name="sh")
+        ch = const.tile([P, 8], F32, name="ch")
+        rr = const.tile([P, 8], F32, name="rr")
+        wt = const.tile([P, 8], F32, name="wt")
+        nc.vector.tensor_scalar_max(out=nm[:], in0=nrm[:], scalar1=1.0e-7)
+        nc.vector.reciprocal(out=rn[:], in_=nm[:])
+        nc.vector.tensor_single_scalar(out=big[:], in_=nrm[:], scalar=1.0e-7, op=ALU.is_gt)
+        nc.vector.scalar_tensor_tensor(out=c1[:], in0=rn[:], scalar=0.5, in1=big[:], op0=ALU.mult, op1=ALU.mult)
+        nc.vector.tensor_scalar(out=c0[:], in0=big[:], scalar1=-1.0, scalar2=1.0, op0=ALU.mult, op1=ALU.add)
+
+        h_transpose(0)
+        h_transpose(1)
+        h_evac(0, 0, "v")
+        nc.vector.tensor_tensor(out=sh[:], in0=ep[:], in1=em[:], op=ALU.subtract)
+        nc.vector.tensor_tensor(out=sh[:], in0=sh[:], in1=c1[:], op=ALU.mult)
+        nc.vector.tensor_tensor(out=rr[:], in0=sh[:], in1=c0[:], op=ALU.add)
+        h_evac(0, 1, "v")
+        nc.vector.tensor_tensor(out=ch[:], in0=ep[:], in1=em[:], op=ALU.add)
+        nc.vector.tensor_scalar_mul(out=wt[:], in0=ch[:], scalar1=0.5)
+        h_quantise(0)
+        h_evac(1, 0, "s")
+        h_evac(1, 1, "s")
+
+        r_bc = const.tile([P, V], F32, name="r_bc")
+        wt_bc = const.tile([P, V], F32, name="wt_bc")
+
+        def spread(vec, dst, h):
+            acc = accp.tile([P, HB], F32, name="bc", tag="acc")
+            for jj in range(4):
+                j = 4 * h + jj
+                nc.tensor.matmul(
+                    out=acc[:, jj * P : (jj + 1) * P],
+                    lhsT=vec[:, j : j + 1].to_broadcast([P, P]),
+                    rhs=ident[:],
+                    start=True,
+                    stop=True,
+                )
+            nc.scalar.copy(out=dst[:, h * HB : (h + 1) * HB], in_=acc[:])
+
+        wg = [const.tile([P, 4 * HB], BF16, name="wg%d" % h, align_bytes=64) for h in range(2)]
+        wc = const.tile([P, V], U32, name="wc", align_bytes=64)
+        wsc = const.tile([P, V], U8, name="wsc", align_bytes=64)
+        tpw = {}
+
+        def w_transpose(q):
+            t = tpp.tile([P, HB], F32, name="tpw", tag="tp")
+            tpw[q] = t
+            for jj in range(2):
+                w32 = wraw[q][:].bitcast(F32)
+                base = jj * (K // 2)
+                for u in range(2):
+                    nc.tensor.transpose(
+                        out=t[:, u * 256 + jj * P : u * 256 + (jj + 1) * P],
+                        in_=w32[:, base + u * P : base + (u + 1) * P],
+                        identity=ident[:],
+                    )
+
+        def w_scale_out(q):
+            h = q // 2
+            nc.vector.tensor_tensor(
+                out=wg[h][:, (q % 2) * 1024 : (q % 2 + 1) * 1024].rearrange("p (v u e) -> p v u e", u=2, e=2),
+                in0=tpw[q][:].bitcast(BF16).rearrange("p (u v e) -> p v u e", u=2, e=2),
+                in1=r_bc[:, q * 256 : (q + 1) * 256].unsqueeze(2).unsqueeze(3).to_broadcast([P, 256, 2, 2]),
+                op=ALU.mult,
+            )
+
+        def w_quantise(h):
+            nc.vector.quantize_mx(
+                out=wc[:, h * HB : (h + 1) * HB].bitcast(FP8X4),
+                scales=wsc[:, h * HB : (h + 1) * HB],
+                in_=wg[h][:],
+            )
+
+        spread(rr, r_bc, 0)
+        w_transpose(0)
+        w_transpose(1)
+        spread(wt, wt_bc, 0)
+        h_quantise(1)
+        w_scale_out(0)
+        w_scale_out(1)
+        w_quantise(0)
+        for g in (2, 3):
+            h_transpose(g)
+            h_evac(g, 0, "s")
+            h_evac(g, 1, "s")
+
+        acc_of = {}
+        x_of = {}
+        a_of = {}
+
+        def width(u):
+            return len(units[u]) * HB
+
+        def mm(u):
+            for k, (i, h) in enumerate(units[u]):
+                g = i // 4
+                cols = slice((i % 4) * P, (i % 4 + 1) * P)
+                acc = accp.tile([P, HB], F32, name="acc", tag="acc")
+                acc_of[(u, k)] = acc
+                nc.tensor.matmul_mx(
+                    out=acc[:],
+                    lhsT=hc[g][:, cols].bitcast(FP8X4),
+                    lhsT_scale=hs[g][:, cols],
+                    rhs=wc[:, h * HB : (h + 1) * HB].bitcast(FP8X4),
+                    rhs_scale=wsc[:, h * HB : (h + 1) * HB],
+                    start=True,
+                    stop=True,
+                )
+
+        def a_c(u):
+            x = xp.tile([P, 4 * HB], F32, name="x", tag="x")
+            x_of[u] = x
+            for k, (i, h) in enumerate(units[u]):
+                nc.vector.scalar_tensor_tensor(
+                    out=x[:, k * HB : (k + 1) * HB],
+                    in0=wt_bc[:, h * HB : (h + 1) * HB],
+                    scalar=ts[:, i : i + 1],
+                    in1=acc_of[(u, k)][:],
+                    op0=ALU.mult,
+                    op1=ALU.subtract,
+                )
+            w = width(u)
+            eng = nc.gpsimd if C_ON_G else nc.vector
+            eng.tensor_scalar(out=x[:, 0:w], in0=x[:, 0:w], scalar1=-1.0, scalar2=1.0e-12, op0=ALU.add, op1=ALU.max)
+
+        def sq(u):
+            a = app.tile([P, 4 * HB], F32, name="a", tag="a")
+            a_of[u] = a
+            x = x_of[u]
+            w = width(u)
+            nc.scalar.activation(out=a[:, 0:w], in_=x[:, 0:w], func=ACT.Sqrt, bias=one[:, 0:1], scale=0.5)
+            nc.scalar.activation(out=x[:, 0:w], in_=x[:, 0:w], func=ACT.Sqrt, scale=0.5)
+
+        def zz(u):
+            w = width(u)
+            nc.vector.tensor_tensor(out=a_of[u][:, 0:w], in0=a_of[u][:, 0:w], in1=x_of[u][:, 0:w], op=ALU.add)
+
+        def ln(u):
+            w = width(u)
+            nc.scalar.activation(out=a_of[u][:, 0:w], in_=a_of[u][:, 0:w], func=ACT.Ln)
+
+        def fin(u):
+            a = a_of[u]
+            w = width(u)
+            nc.vector.scalar_tensor_tensor(
+                out=a[:, 0:w], in0=a[:, 0:w], scalar=m4tau[:, 0:1], in1=a[:, 0:w], op0=ALU.mult, op1=ALU.mult
+            )
+            banks = units[u]
+            i0, h0 = banks[0]
+            if all(h == h0 for (i, h) in banks) and len(banks) > 1:
+                nc.sync.dma_start(
+                    out=out3[:, i0 : i0 + len(banks), h0 * HB : (h0 + 1) * HB],
+                    in_=a[:, 0:w].rearrange("p (i c) -> p i c", c=HB),
+                )
+            else:
+                start = i0 * V + h0 * HB
+                nc.sync.dma_start(out=outv[:, start : start + w], in_=a[:, 0:w])
+
+        nxt = {"t": 4, "q": 2}
+
+        def prep_te():
+            g = nxt["t"]
+            h_transpose(g)
+            h_evac(g, 0, "s")
+            h_evac(g, 1, "s")
+            nxt["t"] = g + 1
+
+        def prep_q():
+            h_quantise(nxt["q"])
+            nxt["q"] = nxt["q"] + 1
+
+        def front(u):
+            if u >= len(units):
+                return
+            need = max(i // 4 for (i, h) in units[u])
+            while nxt["q"] <= need:
+                if nxt["t"] <= nxt["q"]:
+                    prep_te()
+                prep_q()
+            mm(u)
+            a_c(u)
+
+        def extra(step):
+            if step == W1AT:
+                spread(rr, r_bc, 1)
+                w_transpose(2)
+                w_transpose(3)
+                spread(wt, wt_bc, 1)
+                w_scale_out(2)
+                w_scale_out(3)
+                w_quantise(1)
+            if step == TS_LATE_AT:
+                time_coordinate(1, 4)
+            if step >= PREP_FROM and (step - PREP_FROM) % PREP_EVERY == 0:
+                if nxt["q"] < nxt["t"]:
+                    prep_q()
+                if nxt["t"] < 8:
+                    prep_te()
+
+        step = 0
+        for u in range(LA):
+            front(u)
+            extra(step)
+            step += 1
+        u0 = 0
+        for nb in BATCHES:
+            for u in range(u0, u0 + nb):
+                sq(u)
+                front(u + LA)
+                extra(step)
+                step += 1
+                zz(u)
+            for u in range(u0, u0 + nb):
+                ln(u)
+                fin(u)
+            u0 += nb

@@ -20,7 +20,7 @@ NT = NTOK // P
 SLOT = 528
 FMAX = 3.3896e38
 FLOPS = 2 * NTOK * V * K
-C_ON_G = False
+C_ON_G = True
 BATCHES = [10,10]
 LA = 3
 W1AT = 3

@@ -18,26 +18,29 @@ K = 512
 HB = 512
 NT = NTOK // P
 SLOT = 528
-FMAX = 3.3896e38
+FMAX = 3.3895313892515355e38
+CINF = 1.0e4 / FMAX
+XMIN = 1.0 + 2.0 ** -23
+XMAX = 2.0 ** 118
 FLOPS = 2 * NTOK * V * K
-C_ON_G = True
+SANITISE = True
 BATCHES = [10,10]
 LA = 3
-W1AT = 3
-PREP_FROM = 4
-PREP_EVERY = 2
-TS_LATE_AT = 5
+SAN_LEAD = 4
+TE_LAG = 2
+Q_LAG = 1
+K0 = 3
 
 
 def make_units():
-    units = [[(0, 0)], [(1, 0)], [(2, 0), (3, 0)]]
-    units.append([(i, 0) for i in range(4, 8)])
-    units.append([(i, 1) for i in range(0, 4)])
-    units.append([(i, 1) for i in range(4, 8)])
-    for i in range(8, 30, 2):
+    units = [[(0, 0)], [(1, 0)], [(2, 0), (3, 0)], [(i, 1) for i in range(4)]]
+    parent = [(0, 0), (0, 1), (0, 2), (1, 0)]
+    for i in range(4, 30, 2):
+        parent.append((len(units) - 2, 0))
         units.append([(i, 0), (i, 1), (i + 1, 0), (i + 1, 1)])
     units.extend([[(30, 0), (30, 1)], [(31, 0)], [(31, 1)]])
-    return units
+    parent.extend([(15, 0), (15, 2), (15, 3)])
+    return units, parent
 
 
 def tile_geodesiclmheadv2_t_kernel(tc, hidden_states, weight, logit_scale, out):
@@ -46,13 +49,14 @@ def tile_geodesiclmheadv2_t_kernel(tc, hidden_states, weight, logit_scale, out):
     out3 = out.flatten_outer_dims().rearrange("(p i) v -> p i v", i=NT)
     outv = out.flatten_outer_dims().rearrange("(p i) v -> p (i v)", i=NT)
     wv = weight.rearrange("(j p) k -> p j k", p=P)
-    units = make_units()
+    units, parent = make_units()
+    n_units = len(units)
 
     with ExitStack() as ctx:
         const = ctx.enter_context(tc.tile_pool(name="const", bufs=1))
-        hgp = ctx.enter_context(tc.tile_pool(name="hgp", bufs=4))
+        hgp = ctx.enter_context(tc.tile_pool(name="hgp", bufs=3))
         xp = ctx.enter_context(tc.tile_pool(name="xp", bufs=4))
-        app = ctx.enter_context(tc.tile_pool(name="app", bufs=10))
+        app = ctx.enter_context(tc.tile_pool(name="app", bufs=9))
         tpp = ctx.enter_context(tc.psum_pool(name="tpp", bufs=4))
         accp = ctx.enter_context(tc.psum_pool(name="accp", bufs=4))
         ctx.enter_context(tc.manual_schedule())
@@ -62,6 +66,10 @@ def tile_geodesiclmheadv2_t_kernel(tc, hidden_states, weight, logit_scale, out):
         warm = const.tile([P, 1], F32, name="warm")
         make_identity(nc, ident[:])
         nc.vector.memset(one[:], 1.0)
+        half = const.tile([P, 1], F32, name="half")
+        mhalf = const.tile([P, 1], F32, name="mhalf")
+        nc.vector.memset(half[:], 0.5)
+        nc.vector.memset(mhalf[:], -0.5)
         nc.scalar.activation(out=warm[:], in_=one[:], func=ACT.Sqrt)
 
         wraw = [const.tile([P, 2 * K], BF16, name="wraw%d" % a) for a in range(4)]
@@ -80,7 +88,6 @@ def tile_geodesiclmheadv2_t_kernel(tc, hidden_states, weight, logit_scale, out):
                 nc.sync.dma_start(out=ls[:], in_=logit_scale.partition_broadcast(P))
 
         traw = const.tile([P, NT], F32, name="traw")
-        tfin = const.tile([P, NT], F32, name="tfin")
         tcl = const.tile([P, NT], F32, name="tcl")
         tkp = const.tile([P, NT], F32, name="tkp")
         tkn = const.tile([P, NT], F32, name="tkn")
@@ -93,24 +100,50 @@ def tile_geodesiclmheadv2_t_kernel(tc, hidden_states, weight, logit_scale, out):
                     in_=hraw[c][:].rearrange("p (i c) -> p i c", c=SLOT)[:, :, 1:2],
                 )
             s = slice(8 * c0, 8 * c1)
-            nc.gpsimd.tensor_scalar(out=tfin[:, s], in0=traw[:, s], scalar1=0.0, scalar2=0.0, op0=ALU.mult, op1=ALU.is_equal)
+            nc.gpsimd.tensor_scalar(out=tkp[:, s], in0=traw[:, s], scalar1=FMAX, scalar2=CINF, op0=ALU.is_le, op1=ALU.add)
+            nc.gpsimd.tensor_scalar(out=tkn[:, s], in0=traw[:, s], scalar1=-FMAX, scalar2=CINF, op0=ALU.is_ge, op1=ALU.add)
+            nc.gpsimd.tensor_tensor(out=tkp[:, s], in0=tkp[:, s], in1=tkn[:, s], op=ALU.mult)
             nc.gpsimd.tensor_scalar(out=tcl[:, s], in0=traw[:, s], scalar1=-FMAX, scalar2=FMAX, op0=ALU.max, op1=ALU.min)
-            nc.gpsimd.tensor_tensor(out=tcl[:, s], in0=tcl[:, s], in1=tfin[:, s], op=ALU.mult)
-            nc.gpsimd.tensor_scalar(out=tkp[:, s], in0=traw[:, s], scalar1=FMAX, scalar2=1.0e4, op0=ALU.is_gt, op1=ALU.mult)
-            nc.gpsimd.tensor_scalar(out=tkn[:, s], in0=traw[:, s], scalar1=-FMAX, scalar2=-1.0e4, op0=ALU.is_lt, op1=ALU.mult)
-            nc.gpsimd.tensor_tensor(out=tkp[:, s], in0=tkp[:, s], in1=tkn[:, s], op=ALU.add)
-            nc.gpsimd.tensor_tensor(out=ts[:, s], in0=tcl[:, s], in1=tkp[:, s], op=ALU.add)
+            nc.gpsimd.tensor_tensor(out=ts[:, s], in0=tcl[:, s], in1=tkp[:, s], op=ALU.mult)
 
         time_coordinate(0, 1)
         tau = const.tile([P, 1], F32, name="tau")
+        tge = const.tile([P, 1], F32, name="tge")
+        tlt = const.tile([P, 1], F32, name="tlt")
         m4tau = const.tile([P, 1], F32, name="m4tau")
         nc.gpsimd.tensor_scalar(out=tau[:], in0=ls[:], scalar1=0.01, scalar2=2.5, op0=ALU.max, op1=ALU.min)
-        nc.gpsimd.tensor_scalar(out=m4tau[:], in0=tau[:], scalar1=-4.0, scalar2=0.0, op0=ALU.mult, op1=ALU.add)
+        nc.gpsimd.tensor_scalar(out=tge[:], in0=ls[:], scalar1=0.0, scalar2=-4.0, op0=ALU.is_ge, op1=ALU.mult)
+        nc.gpsimd.tensor_scalar(out=tlt[:], in0=ls[:], scalar1=0.0, scalar2=-4.0, op0=ALU.is_lt, op1=ALU.mult)
+        nc.gpsimd.tensor_tensor(out=tge[:], in0=tge[:], in1=tlt[:], op=ALU.add)
+        nc.gpsimd.tensor_tensor(out=m4tau[:], in0=tau[:], in1=tge[:], op=ALU.mult)
 
         hc = [const.tile([P, 4 * P], U32, name="hc%d" % g, align_bytes=64) for g in range(8)]
         hs = [const.tile([P, 4 * P], U8, name="hs%d" % g, align_bytes=64) for g in range(8)]
+        gpos = const.tile([P, 4 * K], BF16, name="gpos")
+        gneg = const.tile([P, 4 * K], BF16, name="gneg")
         hg_of = {}
         tph_of = {}
+
+        def spatial(g):
+            rows = hraw[g // 2][:].rearrange("p (i c) -> p i c", c=SLOT)
+            return rows[:, (g % 2) * 4 : (g % 2) * 4 + 4, 2 : K + 2]
+
+        def sanitise_masks(g):
+            if not SANITISE:
+                return
+            x = spatial(g)
+            gp3 = gpos[:].rearrange("p (i c) -> p i c", c=K)
+            gn3 = gneg[:].rearrange("p (i c) -> p i c", c=K)
+            nc.vector.tensor_scalar(out=gp3, in0=x, scalar1=FMAX, scalar2=CINF, op0=ALU.is_le, op1=ALU.add)
+            nc.vector.tensor_scalar(out=gn3, in0=x, scalar1=-FMAX, scalar2=CINF, op0=ALU.is_ge, op1=ALU.add)
+
+        def sanitise_apply(g):
+            if not SANITISE:
+                return
+            x = spatial(g)
+            nc.vector.tensor_tensor(out=gpos[:], in0=gpos[:], in1=gneg[:], op=ALU.mult)
+            nc.vector.tensor_scalar(out=x, in0=x, scalar1=-FMAX, scalar2=FMAX, op0=ALU.max, op1=ALU.min)
+            nc.vector.tensor_tensor(out=x, in0=x, in1=gpos[:].rearrange("p (i c) -> p i c", c=K), op=ALU.mult)
 
         def h_transpose(g):
             for half in range(2):
@@ -127,16 +160,14 @@ def tile_geodesiclmheadv2_t_kernel(tc, hidden_states, weight, logit_scale, out):
                             identity=ident[:],
                         )
 
-        def h_evac(g, half, eng):
-            if half == 0:
-                hg_of[g] = hgp.tile([P, 16 * P], BF16, name="hg", tag="hg", align_bytes=64)
+        def h_evac(g):
+            hg_of[g] = hgp.tile([P, 16 * P], BF16, name="hg", tag="hg", align_bytes=64)
             hg32 = hg_of[g][:].bitcast(F32).rearrange("p (t u) -> p t u", u=2)
-            dst = hg32[:, half * 256 : (half + 1) * 256, :]
-            src = tph_of[(g, half)][:].rearrange("p (u t) -> p t u", u=2)
-            if eng == "v":
-                nc.vector.tensor_copy(out=dst, in_=src)
-            else:
-                nc.scalar.copy(out=dst, in_=src)
+            for half in range(2):
+                nc.scalar.copy(
+                    out=hg32[:, half * 256 : (half + 1) * 256, :],
+                    in_=tph_of[(g, half)][:].rearrange("p (u t) -> p t u", u=2),
+                )
 
         def h_quantise(g):
             nc.vector.quantize_mx(out=hc[g][:].bitcast(FP8X4), scales=hs[g][:], in_=hg_of[g][:])
@@ -144,23 +175,13 @@ def tile_geodesiclmheadv2_t_kernel(tc, hidden_states, weight, logit_scale, out):
         n2s = const.tile([P, 8], F32, name="n2s")
         n2 = const.tile([P, 8], F32, name="n2")
         junk = const.tile([P, K], BF16, name="junk")
-        sqv = const.tile([P, K], F32, name="sqv")
 
         def wrow(j):
             return wraw[j // 2][:, (j % 2) * K : (j % 2 + 1) * K]
 
-        for j in (0, 1, 4, 5):
+        for j in range(8):
             nc.scalar.activation(out=junk[:], in_=wrow(j), func=ACT.Square, accum_out=n2s[:, j : j + 1])
-        for j in (2, 3, 6, 7):
-            nc.vector.scalar_tensor_tensor(
-                out=sqv[:], in0=wrow(j), scalar=1.0, in1=wrow(j), op0=ALU.mult, op1=ALU.mult,
-                accum_out=n2[:, j : j + 1],
-            )
-        nc.vector.tensor_copy(
-            out=n2[:].rearrange("p (a b) -> p a b", b=4)[:, :, 0:2],
-            in_=n2s[:].rearrange("p (a b) -> p a b", b=4)[:, :, 0:2],
-        )
-        nc.vector.tensor_scalar_max(out=n2[:], in0=n2[:], scalar1=1.0e-30)
+        nc.vector.tensor_scalar_max(out=n2[:], in0=n2s[:], scalar1=1.0e-30)
 
         nrm = const.tile([P, 8], F32, name="nrm")
         ep = const.tile([P, 8], F32, name="ep")
@@ -168,6 +189,7 @@ def tile_geodesiclmheadv2_t_kernel(tc, hidden_states, weight, logit_scale, out):
         nc.scalar.activation(out=nrm[:], in_=n2[:], func=ACT.Sqrt)
         nc.scalar.activation(out=ep[:], in_=nrm[:], func=ACT.Exp)
         nc.scalar.activation(out=em[:], in_=nrm[:], func=ACT.Exp, scale=-1.0)
+        nc.scalar.activation(out=warm[:], in_=one[:], func=ACT.Sqrt)
 
         nm = const.tile([P, 8], F32, name="nm")
         rn = const.tile([P, 8], F32, name="rn")
@@ -184,24 +206,22 @@ def tile_geodesiclmheadv2_t_kernel(tc, hidden_states, weight, logit_scale, out):
         nc.vector.scalar_tensor_tensor(out=c1[:], in0=rn[:], scalar=0.5, in1=big[:], op0=ALU.mult, op1=ALU.mult)
         nc.vector.tensor_scalar(out=c0[:], in0=big[:], scalar1=-1.0, scalar2=1.0, op0=ALU.mult, op1=ALU.add)
 
-        h_transpose(0)
-        h_transpose(1)
-        h_evac(0, 0, "v")
+        sanitise_masks(0)
         nc.vector.tensor_tensor(out=sh[:], in0=ep[:], in1=em[:], op=ALU.subtract)
         nc.vector.tensor_tensor(out=sh[:], in0=sh[:], in1=c1[:], op=ALU.mult)
         nc.vector.tensor_tensor(out=rr[:], in0=sh[:], in1=c0[:], op=ALU.add)
-        h_evac(0, 1, "v")
+        sanitise_apply(0)
         nc.vector.tensor_tensor(out=ch[:], in0=ep[:], in1=em[:], op=ALU.add)
         nc.vector.tensor_scalar_mul(out=wt[:], in0=ch[:], scalar1=0.5)
-        h_quantise(0)
-        h_evac(1, 0, "s")
-        h_evac(1, 1, "s")
 
         r_bc = const.tile([P, V], F32, name="r_bc")
         wt_bc = const.tile([P, V], F32, name="wt_bc")
+        bc_of = {}
 
-        def spread(vec, dst, h):
+        def spread_mm(vec, key):
+            h = key[1]
             acc = accp.tile([P, HB], F32, name="bc", tag="acc")
+            bc_of[key] = acc
             for jj in range(4):
                 j = 4 * h + jj
                 nc.tensor.matmul(
@@ -211,7 +231,10 @@ def tile_geodesiclmheadv2_t_kernel(tc, hidden_states, weight, logit_scale, out):
                     start=True,
                     stop=True,
                 )
-            nc.scalar.copy(out=dst[:, h * HB : (h + 1) * HB], in_=acc[:])
+
+        def spread_copy(dst, key):
+            h = key[1]
+            nc.scalar.copy(out=dst[:, h * HB : (h + 1) * HB], in_=bc_of[key][:])
 
         wg = [const.tile([P, 4 * HB], BF16, name="wg%d" % h, align_bytes=64) for h in range(2)]
         wc = const.tile([P, V], U32, name="wc", align_bytes=64)
@@ -247,36 +270,37 @@ def tile_geodesiclmheadv2_t_kernel(tc, hidden_states, weight, logit_scale, out):
                 in_=wg[h][:],
             )
 
-        spread(rr, r_bc, 0)
+        spread_mm(rr, ("r", 0))
+        spread_copy(r_bc, ("r", 0))
         w_transpose(0)
         w_transpose(1)
-        spread(wt, wt_bc, 0)
-        h_quantise(1)
+        h_transpose(0)
+        spread_mm(wt, ("w", 0))
+        h_evac(0)
+        spread_copy(wt_bc, ("w", 0))
         w_scale_out(0)
         w_scale_out(1)
         w_quantise(0)
-        for g in (2, 3):
-            h_transpose(g)
-            h_evac(g, 0, "s")
-            h_evac(g, 1, "s")
+        h_quantise(0)
 
         acc_of = {}
         x_of = {}
         a_of = {}
 
-        def width(u):
-            return len(units[u]) * HB
+        def cols(u):
+            first = parent[u][1] * HB
+            return slice(first, first + len(units[u]) * HB)
 
         def mm(u):
             for k, (i, h) in enumerate(units[u]):
                 g = i // 4
-                cols = slice((i % 4) * P, (i % 4 + 1) * P)
+                tok = slice((i % 4) * P, (i % 4 + 1) * P)
                 acc = accp.tile([P, HB], F32, name="acc", tag="acc")
                 acc_of[(u, k)] = acc
                 nc.tensor.matmul_mx(
                     out=acc[:],
-                    lhsT=hc[g][:, cols].bitcast(FP8X4),
-                    lhsT_scale=hs[g][:, cols],
+                    lhsT=hc[g][:, tok].bitcast(FP8X4),
+                    lhsT_scale=hs[g][:, tok],
                     rhs=wc[:, h * HB : (h + 1) * HB].bitcast(FP8X4),
                     rhs_scale=wsc[:, h * HB : (h + 1) * HB],
                     start=True,
@@ -284,109 +308,149 @@ def tile_geodesiclmheadv2_t_kernel(tc, hidden_states, weight, logit_scale, out):
                 )
 
         def a_c(u):
-            x = xp.tile([P, 4 * HB], F32, name="x", tag="x")
-            x_of[u] = x
+            t, first = parent[u]
+            if t not in x_of:
+                x_of[t] = xp.tile([P, 4 * HB], F32, name="x", tag="x")
+            x = x_of[t]
             for k, (i, h) in enumerate(units[u]):
                 nc.vector.scalar_tensor_tensor(
-                    out=x[:, k * HB : (k + 1) * HB],
+                    out=x[:, (first + k) * HB : (first + k + 1) * HB],
                     in0=wt_bc[:, h * HB : (h + 1) * HB],
                     scalar=ts[:, i : i + 1],
                     in1=acc_of[(u, k)][:],
                     op0=ALU.mult,
                     op1=ALU.subtract,
                 )
-            w = width(u)
-            eng = nc.gpsimd if C_ON_G else nc.vector
-            eng.tensor_scalar(out=x[:, 0:w], in0=x[:, 0:w], scalar1=-1.0, scalar2=1.0e-12, op0=ALU.add, op1=ALU.max)
+            c = cols(u)
+            nc.vector.tensor_scalar(out=x[:, c], in0=x[:, c], scalar1=XMIN, scalar2=XMAX, op0=ALU.max, op1=ALU.min)
 
         def sq(u):
-            a = app.tile([P, 4 * HB], F32, name="a", tag="a")
-            a_of[u] = a
-            x = x_of[u]
-            w = width(u)
-            nc.scalar.activation(out=a[:, 0:w], in_=x[:, 0:w], func=ACT.Sqrt, bias=one[:, 0:1], scale=0.5)
-            nc.scalar.activation(out=x[:, 0:w], in_=x[:, 0:w], func=ACT.Sqrt, scale=0.5)
+            t = parent[u][0]
+            if t not in a_of:
+                a_of[t] = app.tile([P, 4 * HB], F32, name="a", tag="a")
+            a = a_of[t]
+            x = x_of[t]
+            c = cols(u)
+            nc.scalar.activation(out=a[:, c], in_=x[:, c], func=ACT.Sqrt, bias=half[:, 0:1], scale=0.5)
+            nc.scalar.activation(out=x[:, c], in_=x[:, c], func=ACT.Sqrt, bias=mhalf[:, 0:1], scale=0.5)
 
         def zz(u):
-            w = width(u)
-            nc.vector.tensor_tensor(out=a_of[u][:, 0:w], in0=a_of[u][:, 0:w], in1=x_of[u][:, 0:w], op=ALU.add)
+            t = parent[u][0]
+            c = cols(u)
+            nc.vector.tensor_tensor(out=a_of[t][:, c], in0=a_of[t][:, c], in1=x_of[t][:, c], op=ALU.add)
 
         def ln(u):
-            w = width(u)
-            nc.scalar.activation(out=a_of[u][:, 0:w], in_=a_of[u][:, 0:w], func=ACT.Ln)
+            t = parent[u][0]
+            c = cols(u)
+            nc.scalar.activation(out=a_of[t][:, c], in_=a_of[t][:, c], func=ACT.Ln)
 
         def fin(u):
-            a = a_of[u]
-            w = width(u)
+            a = a_of[parent[u][0]]
+            c = cols(u)
             nc.vector.scalar_tensor_tensor(
-                out=a[:, 0:w], in0=a[:, 0:w], scalar=m4tau[:, 0:1], in1=a[:, 0:w], op0=ALU.mult, op1=ALU.mult
+                out=a[:, c], in0=a[:, c], scalar=m4tau[:, 0:1], in1=a[:, c], op0=ALU.mult, op1=ALU.mult
             )
             banks = units[u]
             i0, h0 = banks[0]
             if all(h == h0 for (i, h) in banks) and len(banks) > 1:
                 nc.sync.dma_start(
                     out=out3[:, i0 : i0 + len(banks), h0 * HB : (h0 + 1) * HB],
-                    in_=a[:, 0:w].rearrange("p (i c) -> p i c", c=HB),
+                    in_=a[:, c].rearrange("p (i c) -> p i c", c=HB),
                 )
             else:
                 start = i0 * V + h0 * HB
-                nc.sync.dma_start(out=outv[:, start : start + w], in_=a[:, 0:w])
+                nc.sync.dma_start(out=outv[:, start : start + len(banks) * HB], in_=a[:, c])
 
-        nxt = {"t": 4, "q": 2}
+        def group_of(u):
+            return max(i // 4 for (i, h) in units[u])
 
-        def prep_te():
-            g = nxt["t"]
+        items = []
+        seen = {"g": 0, "w1": False}
+        for u in range(n_units):
+            if not seen["w1"] and any(h == 1 for (i, h) in units[u]):
+                items.append(("W1", 0))
+                seen["w1"] = True
+            while seen["g"] < group_of(u):
+                seen["g"] += 1
+                items.append(("SAN", seen["g"]))
+            items.append(("AC", u))
+        for r in range(SAN_LEAD):
+            k = 1
+            while k < len(items):
+                if items[k][0] == "SAN" and items[k - 1][0] != "SAN":
+                    items[k - 1], items[k] = items[k], items[k - 1]
+                    k += 1
+                k += 1
+
+        st = {"san": 0, "te": 0, "q": 0, "step": 0, "ts": False, "next": 0}
+        san_step = {}
+        te_step = {}
+        ac_done = set()
+
+        def do_te(g):
             h_transpose(g)
-            h_evac(g, 0, "s")
-            h_evac(g, 1, "s")
-            nxt["t"] = g + 1
+            h_evac(g)
+            st["te"] = g
+            te_step[g] = st["step"]
 
-        def prep_q():
-            h_quantise(nxt["q"])
-            nxt["q"] = nxt["q"] + 1
+        def do_q(g):
+            h_quantise(g)
+            st["q"] = g
 
-        def front(u):
-            if u >= len(units):
-                return
-            need = max(i // 4 for (i, h) in units[u])
-            while nxt["q"] <= need:
-                if nxt["t"] <= nxt["q"]:
-                    prep_te()
-                prep_q()
-            mm(u)
-            a_c(u)
-
-        def extra(step):
-            if step == W1AT:
-                spread(rr, r_bc, 1)
+        def pull_one():
+            kind, n = items[st["next"]]
+            st["next"] += 1
+            if kind == "W1":
+                spread_mm(rr, ("r", 1))
+                spread_copy(r_bc, ("r", 1))
                 w_transpose(2)
                 w_transpose(3)
-                spread(wt, wt_bc, 1)
+                spread_mm(wt, ("w", 1))
+                spread_copy(wt_bc, ("w", 1))
                 w_scale_out(2)
                 w_scale_out(3)
                 w_quantise(1)
-            if step == TS_LATE_AT:
-                time_coordinate(1, 4)
-            if step >= PREP_FROM and (step - PREP_FROM) % PREP_EVERY == 0:
-                if nxt["q"] < nxt["t"]:
-                    prep_q()
-                if nxt["t"] < 8:
-                    prep_te()
+            elif kind == "SAN":
+                sanitise_masks(n)
+                sanitise_apply(n)
+                st["san"] = n
+                san_step[n] = st["step"]
+            else:
+                g = group_of(n)
+                while st["te"] < g:
+                    do_te(st["te"] + 1)
+                while st["q"] < g:
+                    do_q(st["q"] + 1)
+                if not st["ts"] and any(i >= 8 for (i, h) in units[n]):
+                    time_coordinate(1, 4)
+                    st["ts"] = True
+                mm(n)
+                a_c(n)
+                ac_done.add(n)
 
-        step = 0
-        for u in range(LA):
-            front(u)
-            extra(step)
-            step += 1
+        def pull_until(u):
+            while u not in ac_done:
+                pull_one()
+
+        def flush():
+            st["step"] += 1
+            while st["q"] < st["te"] and te_step[st["q"] + 1] + Q_LAG <= st["step"]:
+                do_q(st["q"] + 1)
+            while st["te"] < st["san"] and san_step[st["te"] + 1] + TE_LAG <= st["step"]:
+                do_te(st["te"] + 1)
+
+        for k in range(K0):
+            pull_one()
         u0 = 0
         for nb in BATCHES:
             for u in range(u0, u0 + nb):
+                pull_until(u)
+                flush()
                 sq(u)
-                front(u + LA)
-                extra(step)
-                step += 1
+                pull_until(min(n_units - 1, u + LA))
                 zz(u)
             for u in range(u0, u0 + nb):
+                flush()
                 ln(u)
                 fin(u)
             u0 += nb

@@ -12,445 +12,480 @@ ALU = mybir.AluOpType
 ACT = mybir.ActivationFunctionType
 
 P = 128
-NTOK = 4096
-V = 1024
+TOKENS = 4096
+VOCAB = 1024
 K = 512
-HB = 512
-NT = NTOK // P
+BANK = 512
+TILES = TOKENS // P
+CHUNK = 8
+GROUP = 4
+GROUPS = TILES // GROUP
+W_TILES = VOCAB // P
 SLOT = 528
 FMAX = 3.3895313892515355e38
-CINF = 1.0e4 / FMAX
-XMIN = 1.0 + 2.0 ** -23
-XMAX = 2.0 ** 118
-FLOPS = 2 * NTOK * V * K
-SANITISE = True
-BATCHES = [10,10]
-LA = 3
-SAN_LEAD = 4
-TE_LAG = 2
-Q_LAG = 1
-K0 = 3
+C_INF = 1.0e4 / FMAX
+SUMSQ_MAX = 7.0e3
+FLOPS = 2 * TOKENS * VOCAB * K
+
+BATCHES = (10, 10)
+LOOKAHEAD = 4
+X_TILES = 5
+A_TILES = 9
+SANITISE_LEAD = 4
+TRANSPOSE_LAG = 2
+QUANTISE_LAG = 1
+SCALAR_CLIPS = 7
+FIRST_PULLS = 3
 
 
 def make_units():
-    units = [[(0, 0)], [(1, 0)], [(2, 0), (3, 0)], [(i, 1) for i in range(4)]]
-    parent = [(0, 0), (0, 1), (0, 2), (1, 0)]
-    for i in range(4, 30, 2):
-        parent.append((len(units) - 2, 0))
+    units = [[(0, 0)], [(1, 0)], [(2, 0), (3, 0)], [(i, 1) for i in range(GROUP)]]
+    place = [(0, 0), (0, 1), (0, 2), (1, 0)]
+    for i in range(GROUP, TILES - 2, 2):
+        place.append((len(units) - 2, 0))
         units.append([(i, 0), (i, 1), (i + 1, 0), (i + 1, 1)])
-    units.extend([[(30, 0), (30, 1)], [(31, 0)], [(31, 1)]])
-    parent.extend([(15, 0), (15, 2), (15, 3)])
-    return units, parent
+    last = len(units) - 2
+    units.extend([[(TILES - 2, 0), (TILES - 2, 1)], [(TILES - 1, 0)], [(TILES - 1, 1)]])
+    place.extend([(last, 0), (last, 2), (last, 3)])
+    return units, place
 
 
 def tile_geodesiclmheadv2_t_kernel(tc, hidden_states, weight, logit_scale, out):
     nc = tc.nc
-    hid = hidden_states.flatten_outer_dims().rearrange("(p i) c -> p i c", i=NT)
-    out3 = out.flatten_outer_dims().rearrange("(p i) v -> p i v", i=NT)
-    outv = out.flatten_outer_dims().rearrange("(p i) v -> p (i v)", i=NT)
-    wv = weight.rearrange("(j p) k -> p j k", p=P)
-    units, parent = make_units()
+    hid = hidden_states.flatten_outer_dims().rearrange("(p i) c -> p i c", i=TILES)
+    out_tiles = out.flatten_outer_dims().rearrange("(p i) v -> p i v", i=TILES)
+    out_flat = out.flatten_outer_dims().rearrange("(p i) v -> p (i v)", i=TILES)
+    w_rows = weight.rearrange("(j p) k -> p j k", p=P)
+    units, place = make_units()
     n_units = len(units)
 
     with ExitStack() as ctx:
-        const = ctx.enter_context(tc.tile_pool(name="const", bufs=1))
-        hgp = ctx.enter_context(tc.tile_pool(name="hgp", bufs=3))
-        xp = ctx.enter_context(tc.tile_pool(name="xp", bufs=4))
-        app = ctx.enter_context(tc.tile_pool(name="app", bufs=9))
-        tpp = ctx.enter_context(tc.psum_pool(name="tpp", bufs=4))
-        accp = ctx.enter_context(tc.psum_pool(name="accp", bufs=4))
+        keep = ctx.enter_context(tc.tile_pool(name="keep", bufs=1))
+        grouped_pool = ctx.enter_context(tc.tile_pool(name="grouped", bufs=3))
+        x_pool = ctx.enter_context(tc.tile_pool(name="x", bufs=X_TILES))
+        a_pool = ctx.enter_context(tc.tile_pool(name="a", bufs=A_TILES))
+        turn_pool = ctx.enter_context(tc.psum_pool(name="turn", bufs=4))
+        sum_pool = ctx.enter_context(tc.psum_pool(name="sum", bufs=4))
         ctx.enter_context(tc.manual_schedule())
 
-        ident = const.tile([P, P], F32, name="ident")
-        one = const.tile([P, 1], F32, name="one")
-        warm = const.tile([P, 1], F32, name="warm")
+        ident = keep.tile([P, P], F32, name="ident")
+        one = keep.tile([P, 1], F32, name="one")
+        minus_one = keep.tile([P, 1], F32, name="minus_one")
+        floor_b = keep.tile([P, 1], F32, name="floor_b")
+        scratch = keep.tile([P, 1], F32, name="scratch")
+        ident_bf = keep.tile([P, P], BF16, name="ident_bf")
         make_identity(nc, ident[:])
+        make_identity(nc, ident_bf[:])
         nc.vector.memset(one[:], 1.0)
-        half = const.tile([P, 1], F32, name="half")
-        mhalf = const.tile([P, 1], F32, name="mhalf")
-        nc.vector.memset(half[:], 0.5)
-        nc.vector.memset(mhalf[:], -0.5)
-        nc.scalar.activation(out=warm[:], in_=one[:], func=ACT.Sqrt)
+        nc.vector.memset(minus_one[:], -1.0)
+        nc.vector.memset(floor_b[:], 0.5e-12)
+        nc.scalar.activation(out=scratch[:], in_=one[:], func=ACT.Sqrt)
 
-        wraw = [const.tile([P, 2 * K], BF16, name="wraw%d" % a) for a in range(4)]
-        for a in range(4):
+        w_raw = [keep.tile([P, 2 * K], BF16, name="w_raw%d" % q) for q in range(W_TILES // 2)]
+        for q in range(W_TILES // 2):
             nc.sync.dma_start(
-                out=wraw[a][:].rearrange("p (j k) -> p j k", k=K), in_=wv[:, 2 * a : 2 * a + 2, :]
+                out=w_raw[q][:].rearrange("p (j k) -> p j k", k=K), in_=w_rows[:, 2 * q : 2 * q + 2, :]
             )
-        hraw = [const.tile([P, 8 * SLOT], BF16, name="hraw%d" % c) for c in range(4)]
-        ls = const.tile([P, 1], BF16, name="ls")
-        for c in range(4):
+        h_raw = [keep.tile([P, CHUNK * SLOT], BF16, name="h_raw%d" % c) for c in range(TILES // CHUNK)]
+        scale_raw = keep.tile([P, 1], BF16, name="scale_raw")
+        for c in range(TILES // CHUNK):
             nc.sync.dma_start(
-                out=hraw[c][:].rearrange("p (i c) -> p i c", c=SLOT)[:, :, 1 : K + 2],
-                in_=hid[:, 8 * c : 8 * c + 8, :],
+                out=h_raw[c][:].rearrange("p (i c) -> p i c", c=SLOT)[:, :, 1 : K + 2],
+                in_=hid[:, CHUNK * c : CHUNK * (c + 1), :],
             )
             if c == 0:
-                nc.sync.dma_start(out=ls[:], in_=logit_scale.partition_broadcast(P))
+                nc.sync.dma_start(out=scale_raw[:], in_=logit_scale.partition_broadcast(P))
 
-        traw = const.tile([P, NT], F32, name="traw")
-        tcl = const.tile([P, NT], F32, name="tcl")
-        tkp = const.tile([P, NT], F32, name="tkp")
-        tkn = const.tile([P, NT], F32, name="tkn")
-        ts = const.tile([P, NT], F32, name="ts")
+        def nan_to_num_factor(eng, up, down, x):
+            eng.tensor_scalar(out=up, in0=x, scalar1=FMAX, scalar2=C_INF, op0=ALU.is_le, op1=ALU.add)
+            eng.tensor_scalar(out=down, in0=x, scalar1=-FMAX, scalar2=C_INF, op0=ALU.is_ge, op1=ALU.add)
 
-        def time_coordinate(c0, c1):
+        t_raw = keep.tile([P, TILES], F32, name="t_raw")
+        t_up = keep.tile([P, TILES], F32, name="t_up")
+        t_down = keep.tile([P, TILES], F32, name="t_down")
+        t_coord = keep.tile([P, TILES], F32, name="t_coord")
+
+        def time_coordinates(c0, c1):
             for c in range(c0, c1):
                 nc.gpsimd.tensor_copy(
-                    out=traw[:, 8 * c : 8 * c + 8].unsqueeze(2),
-                    in_=hraw[c][:].rearrange("p (i c) -> p i c", c=SLOT)[:, :, 1:2],
+                    out=t_raw[:, CHUNK * c : CHUNK * (c + 1)].unsqueeze(2),
+                    in_=h_raw[c][:].rearrange("p (i c) -> p i c", c=SLOT)[:, :, 1:2],
                 )
-            s = slice(8 * c0, 8 * c1)
-            nc.gpsimd.tensor_scalar(out=tkp[:, s], in0=traw[:, s], scalar1=FMAX, scalar2=CINF, op0=ALU.is_le, op1=ALU.add)
-            nc.gpsimd.tensor_scalar(out=tkn[:, s], in0=traw[:, s], scalar1=-FMAX, scalar2=CINF, op0=ALU.is_ge, op1=ALU.add)
-            nc.gpsimd.tensor_tensor(out=tkp[:, s], in0=tkp[:, s], in1=tkn[:, s], op=ALU.mult)
-            nc.gpsimd.tensor_scalar(out=tcl[:, s], in0=traw[:, s], scalar1=-FMAX, scalar2=FMAX, op0=ALU.max, op1=ALU.min)
-            nc.gpsimd.tensor_tensor(out=ts[:, s], in0=tcl[:, s], in1=tkp[:, s], op=ALU.mult)
+            s = slice(CHUNK * c0, CHUNK * c1)
+            nan_to_num_factor(nc.gpsimd, t_up[:, s], t_down[:, s], t_raw[:, s])
+            nc.gpsimd.tensor_tensor(out=t_up[:, s], in0=t_up[:, s], in1=t_down[:, s], op=ALU.mult)
+            nc.gpsimd.tensor_scalar(
+                out=t_raw[:, s], in0=t_raw[:, s], scalar1=-FMAX, scalar2=FMAX, op0=ALU.max, op1=ALU.min
+            )
+            nc.gpsimd.tensor_tensor(out=t_coord[:, s], in0=t_raw[:, s], in1=t_up[:, s], op=ALU.mult)
 
-        time_coordinate(0, 1)
-        tau = const.tile([P, 1], F32, name="tau")
-        tge = const.tile([P, 1], F32, name="tge")
-        tlt = const.tile([P, 1], F32, name="tlt")
-        m4tau = const.tile([P, 1], F32, name="m4tau")
-        nc.gpsimd.tensor_scalar(out=tau[:], in0=ls[:], scalar1=0.01, scalar2=2.5, op0=ALU.max, op1=ALU.min)
-        nc.gpsimd.tensor_scalar(out=tge[:], in0=ls[:], scalar1=0.0, scalar2=-4.0, op0=ALU.is_ge, op1=ALU.mult)
-        nc.gpsimd.tensor_scalar(out=tlt[:], in0=ls[:], scalar1=0.0, scalar2=-4.0, op0=ALU.is_lt, op1=ALU.mult)
-        nc.gpsimd.tensor_tensor(out=tge[:], in0=tge[:], in1=tlt[:], op=ALU.add)
-        nc.gpsimd.tensor_tensor(out=m4tau[:], in0=tau[:], in1=tge[:], op=ALU.mult)
+        time_coordinates(0, 1)
+        tau = keep.tile([P, 1], F32, name="tau")
+        not_neg = keep.tile([P, 1], F32, name="not_neg")
+        neg = keep.tile([P, 1], F32, name="neg")
+        minus_4tau = keep.tile([P, 1], F32, name="minus_4tau")
+        nc.gpsimd.tensor_scalar(out=tau[:], in0=scale_raw[:], scalar1=0.01, scalar2=2.5, op0=ALU.max, op1=ALU.min)
+        nc.gpsimd.tensor_scalar(out=not_neg[:], in0=scale_raw[:], scalar1=0.0, scalar2=-4.0, op0=ALU.is_ge, op1=ALU.mult)
+        nc.gpsimd.tensor_scalar(out=neg[:], in0=scale_raw[:], scalar1=0.0, scalar2=-4.0, op0=ALU.is_lt, op1=ALU.mult)
+        nc.gpsimd.tensor_tensor(out=not_neg[:], in0=not_neg[:], in1=neg[:], op=ALU.add)
+        nc.gpsimd.tensor_tensor(out=minus_4tau[:], in0=tau[:], in1=not_neg[:], op=ALU.mult)
 
-        hc = [const.tile([P, 4 * P], U32, name="hc%d" % g, align_bytes=64) for g in range(8)]
-        hs = [const.tile([P, 4 * P], U8, name="hs%d" % g, align_bytes=64) for g in range(8)]
-        gpos = const.tile([P, 4 * K], BF16, name="gpos")
-        gneg = const.tile([P, 4 * K], BF16, name="gneg")
-        hg_of = {}
-        tph_of = {}
+        h_codes = [keep.tile([P, GROUP * P], U32, name="h_codes%d" % g, align_bytes=64) for g in range(GROUPS)]
+        h_scales = [keep.tile([P, GROUP * P], U8, name="h_scales%d" % g, align_bytes=64) for g in range(GROUPS)]
+        factor_up = keep.tile([P, CHUNK * K], BF16, name="factor_up")
+        factor_down = keep.tile([P, CHUNK * K], BF16, name="factor_down")
+        grouped_of = {}
+        turned_of = {}
 
-        def spatial(g):
-            rows = hraw[g // 2][:].rearrange("p (i c) -> p i c", c=SLOT)
-            return rows[:, (g % 2) * 4 : (g % 2) * 4 + 4, 2 : K + 2]
+        def sanitise_factor(g0, g1):
+            n = (g1 - g0) * GROUP
+            first = (g0 % 2) * GROUP
+            x = h_raw[g0 // 2][:].rearrange("p (i c) -> p i c", c=SLOT)[:, first : first + n, 2 : K + 2]
+            up = factor_up[:, 0 : n * K].rearrange("p (i c) -> p i c", c=K)
+            down = factor_down[:, 0 : n * K].rearrange("p (i c) -> p i c", c=K)
+            nan_to_num_factor(nc.vector, up, down, x)
 
-        def sanitise_masks(g):
-            if not SANITISE:
-                return
-            x = spatial(g)
-            gp3 = gpos[:].rearrange("p (i c) -> p i c", c=K)
-            gn3 = gneg[:].rearrange("p (i c) -> p i c", c=K)
-            nc.vector.tensor_scalar(out=gp3, in0=x, scalar1=FMAX, scalar2=CINF, op0=ALU.is_le, op1=ALU.add)
-            nc.vector.tensor_scalar(out=gn3, in0=x, scalar1=-FMAX, scalar2=CINF, op0=ALU.is_ge, op1=ALU.add)
-
-        def sanitise_apply(g):
-            if not SANITISE:
-                return
-            x = spatial(g)
-            nc.vector.tensor_tensor(out=gpos[:], in0=gpos[:], in1=gneg[:], op=ALU.mult)
+        def sanitise_apply(g0, g1):
+            n = (g1 - g0) * GROUP
+            first = (g0 % 2) * GROUP
+            x = h_raw[g0 // 2][:].rearrange("p (i c) -> p i c", c=SLOT)[:, first : first + n, 2 : K + 2]
+            nc.vector.tensor_tensor(
+                out=factor_up[:, 0 : n * K], in0=factor_up[:, 0 : n * K], in1=factor_down[:, 0 : n * K], op=ALU.mult
+            )
             nc.vector.tensor_scalar(out=x, in0=x, scalar1=-FMAX, scalar2=FMAX, op0=ALU.max, op1=ALU.min)
-            nc.vector.tensor_tensor(out=x, in0=x, in1=gpos[:].rearrange("p (i c) -> p i c", c=K), op=ALU.mult)
+            nc.vector.tensor_tensor(
+                out=x, in0=x, in1=factor_up[:, 0 : n * K].rearrange("p (i c) -> p i c", c=K), op=ALU.mult
+            )
 
         def h_transpose(g):
-            for half in range(2):
-                tph = tpp.tile([P, HB], F32, name="tph", tag="tp")
-                tph_of[(g, half)] = tph
+            for pair in range(2):
+                turned = turn_pool.tile([P, BANK], F32, name="turned", tag="turn")
+                turned_of[(g, pair)] = turned
                 for ii in range(2):
-                    i = 4 * g + 2 * half + ii
-                    h32 = hraw[i // 8][:].bitcast(F32)
-                    base = (i % 8) * (SLOT // 2) + 1
+                    i = GROUP * g + 2 * pair + ii
+                    words = h_raw[i // CHUNK][:].bitcast(F32)
+                    base = (i % CHUNK) * (SLOT // 2) + 1
                     for u in range(2):
                         nc.tensor.transpose(
-                            out=tph[:, u * 256 + ii * P : u * 256 + (ii + 1) * P],
-                            in_=h32[:, base + u * P : base + (u + 1) * P],
+                            out=turned[:, u * 2 * P + ii * P : u * 2 * P + (ii + 1) * P],
+                            in_=words[:, base + u * P : base + (u + 1) * P],
                             identity=ident[:],
                         )
 
-        def h_evac(g):
-            hg_of[g] = hgp.tile([P, 16 * P], BF16, name="hg", tag="hg", align_bytes=64)
-            hg32 = hg_of[g][:].bitcast(F32).rearrange("p (t u) -> p t u", u=2)
-            for half in range(2):
+        def h_copy_out(g):
+            grouped_of[g] = grouped_pool.tile([P, GROUP * K], BF16, name="grouped", tag="grouped", align_bytes=64)
+            words = grouped_of[g][:].bitcast(F32).rearrange("p (t u) -> p t u", u=2)
+            for pair in range(2):
                 nc.scalar.copy(
-                    out=hg32[:, half * 256 : (half + 1) * 256, :],
-                    in_=tph_of[(g, half)][:].rearrange("p (u t) -> p t u", u=2),
+                    out=words[:, pair * 2 * P : (pair + 1) * 2 * P, :],
+                    in_=turned_of[(g, pair)][:].rearrange("p (u t) -> p t u", u=2),
                 )
 
         def h_quantise(g):
-            nc.vector.quantize_mx(out=hc[g][:].bitcast(FP8X4), scales=hs[g][:], in_=hg_of[g][:])
+            nc.vector.quantize_mx(out=h_codes[g][:].bitcast(FP8X4), scales=h_scales[g][:], in_=grouped_of[g][:])
 
-        n2s = const.tile([P, 8], F32, name="n2s")
-        n2 = const.tile([P, 8], F32, name="n2")
-        junk = const.tile([P, K], BF16, name="junk")
+        sumsq_s = keep.tile([P, W_TILES], F32, name="sumsq_s")
+        sumsq = keep.tile([P, W_TILES], F32, name="sumsq")
+        squares_s = keep.tile([P, K], BF16, name="squares_s")
+        squares_v = keep.tile([P, K], F32, name="squares_v")
 
-        def wrow(j):
-            return wraw[j // 2][:, (j % 2) * K : (j % 2 + 1) * K]
+        def w_row_tile(j):
+            return w_raw[j // 2][:, (j % 2) * K : (j % 2 + 1) * K]
 
-        for j in range(8):
-            nc.scalar.activation(out=junk[:], in_=wrow(j), func=ACT.Square, accum_out=n2s[:, j : j + 1])
-        nc.vector.tensor_scalar_max(out=n2[:], in0=n2s[:], scalar1=1.0e-30)
+        for j in (0, 1, 4, 5):
+            nc.scalar.activation(out=squares_s[:], in_=w_row_tile(j), func=ACT.Square, accum_out=sumsq_s[:, j : j + 1])
+        for j in (2, 3, 6, 7):
+            nc.vector.scalar_tensor_tensor(
+                out=squares_v[:], in0=w_row_tile(j), scalar=1.0, in1=w_row_tile(j), op0=ALU.mult, op1=ALU.mult,
+                accum_out=sumsq[:, j : j + 1],
+            )
+        nc.vector.tensor_copy(
+            out=sumsq[:].rearrange("p (a b) -> p a b", b=4)[:, :, 0:2],
+            in_=sumsq_s[:].rearrange("p (a b) -> p a b", b=4)[:, :, 0:2],
+        )
+        row_ok = keep.tile([P, W_TILES], F32, name="row_ok")
+        nc.vector.tensor_single_scalar(out=row_ok[:], in_=sumsq[:], scalar=FMAX, op=ALU.is_le)
+        nc.vector.tensor_scalar(out=sumsq[:], in0=sumsq[:], scalar1=1.0e-30, scalar2=SUMSQ_MAX, op0=ALU.max, op1=ALU.min)
 
-        nrm = const.tile([P, 8], F32, name="nrm")
-        ep = const.tile([P, 8], F32, name="ep")
-        em = const.tile([P, 8], F32, name="em")
-        nc.scalar.activation(out=nrm[:], in_=n2[:], func=ACT.Sqrt)
-        nc.scalar.activation(out=ep[:], in_=nrm[:], func=ACT.Exp)
-        nc.scalar.activation(out=em[:], in_=nrm[:], func=ACT.Exp, scale=-1.0)
-        nc.scalar.activation(out=warm[:], in_=one[:], func=ACT.Sqrt)
+        norm = keep.tile([P, W_TILES], F32, name="norm")
+        e_plus = keep.tile([P, W_TILES], F32, name="e_plus")
+        e_minus = keep.tile([P, W_TILES], F32, name="e_minus")
+        nc.scalar.activation(out=norm[:], in_=sumsq[:], func=ACT.Sqrt)
+        nc.scalar.activation(out=e_plus[:], in_=norm[:], func=ACT.Exp)
+        nc.scalar.activation(out=e_minus[:], in_=norm[:], func=ACT.Exp, scale=-1.0)
+        nc.scalar.activation(out=scratch[:], in_=one[:], func=ACT.Sqrt)
 
-        nm = const.tile([P, 8], F32, name="nm")
-        rn = const.tile([P, 8], F32, name="rn")
-        big = const.tile([P, 8], F32, name="big")
-        c1 = const.tile([P, 8], F32, name="c1")
-        c0 = const.tile([P, 8], F32, name="c0")
-        sh = const.tile([P, 8], F32, name="sh")
-        ch = const.tile([P, 8], F32, name="ch")
-        rr = const.tile([P, 8], F32, name="rr")
-        wt = const.tile([P, 8], F32, name="wt")
-        nc.vector.tensor_scalar_max(out=nm[:], in0=nrm[:], scalar1=1.0e-7)
-        nc.vector.reciprocal(out=rn[:], in_=nm[:])
-        nc.vector.tensor_single_scalar(out=big[:], in_=nrm[:], scalar=1.0e-7, op=ALU.is_gt)
-        nc.vector.scalar_tensor_tensor(out=c1[:], in0=rn[:], scalar=0.5, in1=big[:], op0=ALU.mult, op1=ALU.mult)
-        nc.vector.tensor_scalar(out=c0[:], in0=big[:], scalar1=-1.0, scalar2=1.0, op0=ALU.mult, op1=ALU.add)
+        floor_n = keep.tile([P, W_TILES], F32, name="floor_n")
+        slope = keep.tile([P, W_TILES], F32, name="slope")
+        offset = keep.tile([P, W_TILES], F32, name="offset")
+        large = keep.tile([P, W_TILES], F32, name="large")
+        diff = keep.tile([P, W_TILES], F32, name="diff")
+        total = keep.tile([P, W_TILES], F32, name="total")
+        r_col = keep.tile([P, W_TILES], F32, name="r_col")
+        cosh_col = keep.tile([P, W_TILES], F32, name="cosh_col")
+        nc.vector.tensor_scalar_max(out=floor_n[:], in0=norm[:], scalar1=1.0e-7)
+        nc.vector.reciprocal(out=slope[:], in_=floor_n[:])
+        nc.vector.tensor_single_scalar(out=large[:], in_=norm[:], scalar=1.0e-7, op=ALU.is_gt)
+        nc.vector.scalar_tensor_tensor(out=slope[:], in0=slope[:], scalar=0.5, in1=large[:], op0=ALU.mult, op1=ALU.mult)
+        nc.vector.tensor_tensor(out=slope[:], in0=slope[:], in1=row_ok[:], op=ALU.mult)
+        nc.vector.scalar_tensor_tensor(out=offset[:], in0=large[:], scalar=-1.0, in1=row_ok[:], op0=ALU.mult, op1=ALU.add)
+        nc.vector.tensor_scalar_max(out=offset[:], in0=offset[:], scalar1=0.0)
+        for q in range(W_TILES // 2):
+            nc.vector.tensor_scalar(out=w_raw[q][:], in0=w_raw[q][:], scalar1=-FMAX, scalar2=FMAX, op0=ALU.max, op1=ALU.min)
 
-        sanitise_masks(0)
-        nc.vector.tensor_tensor(out=sh[:], in0=ep[:], in1=em[:], op=ALU.subtract)
-        nc.vector.tensor_tensor(out=sh[:], in0=sh[:], in1=c1[:], op=ALU.mult)
-        nc.vector.tensor_tensor(out=rr[:], in0=sh[:], in1=c0[:], op=ALU.add)
-        sanitise_apply(0)
-        nc.vector.tensor_tensor(out=ch[:], in0=ep[:], in1=em[:], op=ALU.add)
-        nc.vector.tensor_scalar_mul(out=wt[:], in0=ch[:], scalar1=0.5)
+        sanitise_factor(0, 1)
+        nc.vector.tensor_tensor(out=diff[:], in0=e_plus[:], in1=e_minus[:], op=ALU.subtract)
+        nc.vector.tensor_tensor(out=diff[:], in0=diff[:], in1=slope[:], op=ALU.mult)
+        nc.vector.tensor_tensor(out=r_col[:], in0=diff[:], in1=offset[:], op=ALU.add)
+        sanitise_apply(0, 1)
+        nc.vector.tensor_tensor(out=total[:], in0=e_plus[:], in1=e_minus[:], op=ALU.add)
+        nc.vector.scalar_tensor_tensor(out=cosh_col[:], in0=total[:], scalar=0.5, in1=row_ok[:], op0=ALU.mult, op1=ALU.mult)
 
-        r_bc = const.tile([P, V], F32, name="r_bc")
-        wt_bc = const.tile([P, V], F32, name="wt_bc")
-        bc_of = {}
+        cosh_row = keep.tile([P, VOCAB], F32, name="cosh_row")
+        spread_of = {}
 
-        def spread_mm(vec, key):
+        def spread(column, key):
             h = key[1]
-            acc = accp.tile([P, HB], F32, name="bc", tag="acc")
-            bc_of[key] = acc
+            bank = sum_pool.tile([P, BANK], F32, name="spread", tag="sum")
+            spread_of[key] = bank
             for jj in range(4):
                 j = 4 * h + jj
                 nc.tensor.matmul(
-                    out=acc[:, jj * P : (jj + 1) * P],
-                    lhsT=vec[:, j : j + 1].to_broadcast([P, P]),
+                    out=bank[:, jj * P : (jj + 1) * P],
+                    lhsT=column[:, j : j + 1].to_broadcast([P, P]),
                     rhs=ident[:],
                     start=True,
                     stop=True,
                 )
 
-        def spread_copy(dst, key):
+        def spread_copy(row, key):
             h = key[1]
-            nc.scalar.copy(out=dst[:, h * HB : (h + 1) * HB], in_=bc_of[key][:])
+            nc.scalar.copy(out=row[:, h * BANK : (h + 1) * BANK], in_=spread_of[key][:])
 
-        wg = [const.tile([P, 4 * HB], BF16, name="wg%d" % h, align_bytes=64) for h in range(2)]
-        wc = const.tile([P, V], U32, name="wc", align_bytes=64)
-        wsc = const.tile([P, V], U8, name="wsc", align_bytes=64)
-        tpw = {}
+        w_space = keep.tile([P, W_TILES * K], BF16, name="w_space")
+        w_grouped = [keep.tile([P, 4 * BANK], BF16, name="w_grouped%d" % h, align_bytes=64) for h in range(2)]
+        w_codes = keep.tile([P, VOCAB], U32, name="w_codes", align_bytes=64)
+        w_scales = keep.tile([P, VOCAB], U8, name="w_scales", align_bytes=64)
+        w_turned = {}
+
+        def w_scale(j):
+            nc.scalar.activation(
+                out=w_space[:, j * K : (j + 1) * K].rearrange("p (u e q) -> p u e q", u=2, e=2),
+                in_=w_row_tile(j).rearrange("p (u q e) -> p u e q", u=2, e=2),
+                func=ACT.Copy,
+                scale=r_col[:, j : j + 1],
+            )
 
         def w_transpose(q):
-            t = tpp.tile([P, HB], F32, name="tpw", tag="tp")
-            tpw[q] = t
+            turned = turn_pool.tile([P, 2 * BANK], BF16, name="w_turned", tag="turn")
+            w_turned[q] = turned
             for jj in range(2):
-                w32 = wraw[q][:].bitcast(F32)
-                base = jj * (K // 2)
-                for u in range(2):
+                for t in range(4):
                     nc.tensor.transpose(
-                        out=t[:, u * 256 + jj * P : u * 256 + (jj + 1) * P],
-                        in_=w32[:, base + u * P : base + (u + 1) * P],
-                        identity=ident[:],
+                        out=turned[:, (jj * 4 + t) * P : (jj * 4 + t + 1) * P],
+                        in_=w_space[:, (2 * q + jj) * K + t * P : (2 * q + jj) * K + (t + 1) * P],
+                        identity=ident_bf[:],
                     )
 
-        def w_scale_out(q):
-            h = q // 2
-            nc.vector.tensor_tensor(
-                out=wg[h][:, (q % 2) * 1024 : (q % 2 + 1) * 1024].rearrange("p (v u e) -> p v u e", u=2, e=2),
-                in0=tpw[q][:].bitcast(BF16).rearrange("p (u v e) -> p v u e", u=2, e=2),
-                in1=r_bc[:, q * 256 : (q + 1) * 256].unsqueeze(2).unsqueeze(3).to_broadcast([P, 256, 2, 2]),
-                op=ALU.mult,
+        def w_copy_out(q):
+            nc.scalar.copy(
+                out=w_grouped[q // 2][:, (q % 2) * 2 * BANK : (q % 2 + 1) * 2 * BANK].rearrange(
+                    "p (j v t) -> p j v t", j=2, t=4
+                ),
+                in_=w_turned[q][:].rearrange("p (j t v) -> p j v t", j=2, t=4),
             )
 
         def w_quantise(h):
             nc.vector.quantize_mx(
-                out=wc[:, h * HB : (h + 1) * HB].bitcast(FP8X4),
-                scales=wsc[:, h * HB : (h + 1) * HB],
-                in_=wg[h][:],
+                out=w_codes[:, h * BANK : (h + 1) * BANK].bitcast(FP8X4),
+                scales=w_scales[:, h * BANK : (h + 1) * BANK],
+                in_=w_grouped[h][:],
             )
 
-        spread_mm(rr, ("r", 0))
-        spread_copy(r_bc, ("r", 0))
-        w_transpose(0)
-        w_transpose(1)
-        h_transpose(0)
-        spread_mm(wt, ("w", 0))
-        h_evac(0)
-        spread_copy(wt_bc, ("w", 0))
-        w_scale_out(0)
-        w_scale_out(1)
-        w_quantise(0)
+        def w_side(h):
+            for j in range(4 * h, 4 * h + 4):
+                w_scale(j)
+            w_transpose(2 * h)
+            w_transpose(2 * h + 1)
+            if h == 0:
+                h_transpose(0)
+            spread(cosh_col, ("cosh", h))
+            w_copy_out(2 * h)
+            w_copy_out(2 * h + 1)
+            if h == 0:
+                h_copy_out(0)
+            spread_copy(cosh_row, ("cosh", h))
+            w_quantise(h)
+
+        w_side(0)
         h_quantise(0)
 
-        acc_of = {}
+        dot_of = {}
         x_of = {}
         a_of = {}
 
-        def cols(u):
-            first = parent[u][1] * HB
-            return slice(first, first + len(units[u]) * HB)
+        def columns(u):
+            first = place[u][1] * BANK
+            return slice(first, first + len(units[u]) * BANK)
 
-        def mm(u):
+        def dot(u):
             for k, (i, h) in enumerate(units[u]):
-                g = i // 4
-                tok = slice((i % 4) * P, (i % 4 + 1) * P)
-                acc = accp.tile([P, HB], F32, name="acc", tag="acc")
-                acc_of[(u, k)] = acc
+                g = i // GROUP
+                tokens = slice((i % GROUP) * P, (i % GROUP + 1) * P)
+                bank = sum_pool.tile([P, BANK], F32, name="dot", tag="sum")
+                dot_of[(u, k)] = bank
                 nc.tensor.matmul_mx(
-                    out=acc[:],
-                    lhsT=hc[g][:, tok].bitcast(FP8X4),
-                    lhsT_scale=hs[g][:, tok],
-                    rhs=wc[:, h * HB : (h + 1) * HB].bitcast(FP8X4),
-                    rhs_scale=wsc[:, h * HB : (h + 1) * HB],
+                    out=bank[:],
+                    lhsT=h_codes[g][:, tokens].bitcast(FP8X4),
+                    lhsT_scale=h_scales[g][:, tokens],
+                    rhs=w_codes[:, h * BANK : (h + 1) * BANK].bitcast(FP8X4),
+                    rhs_scale=w_scales[:, h * BANK : (h + 1) * BANK],
                     start=True,
                     stop=True,
                 )
 
-        def a_c(u):
-            t, first = parent[u]
-            if t not in x_of:
-                x_of[t] = xp.tile([P, 4 * HB], F32, name="x", tag="x")
-            x = x_of[t]
+        def make_x(u):
+            tile_no, first = place[u]
+            if tile_no not in x_of:
+                x_of[tile_no] = x_pool.tile([P, 4 * BANK], F32, name="x", tag="x")
+            x = x_of[tile_no]
             for k, (i, h) in enumerate(units[u]):
                 nc.vector.scalar_tensor_tensor(
-                    out=x[:, (first + k) * HB : (first + k + 1) * HB],
-                    in0=wt_bc[:, h * HB : (h + 1) * HB],
-                    scalar=ts[:, i : i + 1],
-                    in1=acc_of[(u, k)][:],
+                    out=x[:, (first + k) * BANK : (first + k + 1) * BANK],
+                    in0=cosh_row[:, h * BANK : (h + 1) * BANK],
+                    scalar=t_coord[:, i : i + 1],
+                    in1=dot_of[(u, k)][:],
                     op0=ALU.mult,
                     op1=ALU.subtract,
                 )
-            c = cols(u)
-            nc.vector.tensor_scalar(out=x[:, c], in0=x[:, c], scalar1=XMIN, scalar2=XMAX, op0=ALU.max, op1=ALU.min)
+            if u >= SCALAR_CLIPS:
+                c = columns(u)
+                nc.vector.tensor_scalar(out=x[:, c], in0=x[:, c], scalar1=-1.0, scalar2=0.0, op0=ALU.add, op1=ALU.max)
 
-        def sq(u):
-            t = parent[u][0]
-            if t not in a_of:
-                a_of[t] = app.tile([P, 4 * HB], F32, name="a", tag="a")
-            a = a_of[t]
-            x = x_of[t]
-            c = cols(u)
-            nc.scalar.activation(out=a[:, c], in_=x[:, c], func=ACT.Sqrt, bias=half[:, 0:1], scale=0.5)
-            nc.scalar.activation(out=x[:, c], in_=x[:, c], func=ACT.Sqrt, bias=mhalf[:, 0:1], scale=0.5)
+        def roots(u):
+            tile_no = place[u][0]
+            if tile_no not in a_of:
+                a_of[tile_no] = a_pool.tile([P, 4 * BANK], F32, name="a", tag="a")
+            a = a_of[tile_no]
+            x = x_of[tile_no]
+            c = columns(u)
+            if u < SCALAR_CLIPS:
+                nc.scalar.activation(out=x[:, c], in_=x[:, c], func=ACT.Relu, bias=minus_one[:, 0:1])
+            nc.scalar.activation(out=a[:, c], in_=x[:, c], func=ACT.Sqrt, bias=one[:, 0:1], scale=0.5)
+            nc.scalar.activation(out=x[:, c], in_=x[:, c], func=ACT.Sqrt, bias=floor_b[:, 0:1], scale=0.5)
 
-        def zz(u):
-            t = parent[u][0]
-            c = cols(u)
-            nc.vector.tensor_tensor(out=a_of[t][:, c], in0=a_of[t][:, c], in1=x_of[t][:, c], op=ALU.add)
+        def add_roots(u):
+            tile_no = place[u][0]
+            c = columns(u)
+            nc.vector.tensor_tensor(out=a_of[tile_no][:, c], in0=a_of[tile_no][:, c], in1=x_of[tile_no][:, c], op=ALU.add)
 
-        def ln(u):
-            t = parent[u][0]
-            c = cols(u)
-            nc.scalar.activation(out=a_of[t][:, c], in_=a_of[t][:, c], func=ACT.Ln)
+        def logarithm(u):
+            a = a_of[place[u][0]]
+            c = columns(u)
+            nc.scalar.activation(out=a[:, c], in_=a[:, c], func=ACT.Ln)
 
-        def fin(u):
-            a = a_of[parent[u][0]]
-            c = cols(u)
+        def finish(u):
+            a = a_of[place[u][0]]
+            c = columns(u)
             nc.vector.scalar_tensor_tensor(
-                out=a[:, c], in0=a[:, c], scalar=m4tau[:, 0:1], in1=a[:, c], op0=ALU.mult, op1=ALU.mult
+                out=a[:, c], in0=a[:, c], scalar=minus_4tau[:, 0:1], in1=a[:, c], op0=ALU.mult, op1=ALU.mult
             )
             banks = units[u]
             i0, h0 = banks[0]
-            if all(h == h0 for (i, h) in banks) and len(banks) > 1:
+            if len(banks) > 1 and all(h == h0 for (i, h) in banks):
                 nc.sync.dma_start(
-                    out=out3[:, i0 : i0 + len(banks), h0 * HB : (h0 + 1) * HB],
-                    in_=a[:, c].rearrange("p (i c) -> p i c", c=HB),
+                    out=out_tiles[:, i0 : i0 + len(banks), h0 * BANK : (h0 + 1) * BANK],
+                    in_=a[:, c].rearrange("p (i c) -> p i c", c=BANK),
                 )
             else:
-                start = i0 * V + h0 * HB
-                nc.sync.dma_start(out=outv[:, start : start + len(banks) * HB], in_=a[:, c])
+                start = i0 * VOCAB + h0 * BANK
+                nc.sync.dma_start(out=out_flat[:, start : start + len(banks) * BANK], in_=a[:, c])
 
         def group_of(u):
-            return max(i // 4 for (i, h) in units[u])
+            return max(i // GROUP for (i, h) in units[u])
 
-        items = []
-        seen = {"g": 0, "w1": False}
+        queue = []
+        sanitised = 0
+        second_side = False
         for u in range(n_units):
-            if not seen["w1"] and any(h == 1 for (i, h) in units[u]):
-                items.append(("W1", 0))
-                seen["w1"] = True
-            while seen["g"] < group_of(u):
-                seen["g"] += 1
-                items.append(("SAN", seen["g"]))
-            items.append(("AC", u))
-        for r in range(SAN_LEAD):
+            if not second_side and any(h == 1 for (i, h) in units[u]):
+                queue.append(("w_side", 1, 1))
+                second_side = True
+            if sanitised < group_of(u):
+                upto = sanitised + 1 if sanitised == 0 else sanitised + 2
+                queue.append(("sanitise", sanitised + 1, upto + 1))
+                sanitised = upto
+            queue.append(("x", u, u))
+        for r in range(SANITISE_LEAD):
             k = 1
-            while k < len(items):
-                if items[k][0] == "SAN" and items[k - 1][0] != "SAN":
-                    items[k - 1], items[k] = items[k], items[k - 1]
+            while k < len(queue):
+                if queue[k][0] == "sanitise" and queue[k - 1][0] != "sanitise":
+                    queue[k - 1], queue[k] = queue[k], queue[k - 1]
                     k += 1
                 k += 1
 
-        st = {"san": 0, "te": 0, "q": 0, "step": 0, "ts": False, "next": 0}
-        san_step = {}
-        te_step = {}
-        ac_done = set()
+        state = {"sanitised": 0, "turned": 0, "quantised": 0, "step": 0, "late_t": False, "next": 0}
+        sanitise_step = {}
+        turn_step = {}
+        x_made = set()
 
-        def do_te(g):
+        def turn(g):
             h_transpose(g)
-            h_evac(g)
-            st["te"] = g
-            te_step[g] = st["step"]
+            h_copy_out(g)
+            state["turned"] = g
+            turn_step[g] = state["step"]
 
-        def do_q(g):
+        def quantise(g):
             h_quantise(g)
-            st["q"] = g
+            state["quantised"] = g
 
-        def pull_one():
-            kind, n = items[st["next"]]
-            st["next"] += 1
-            if kind == "W1":
-                spread_mm(rr, ("r", 1))
-                spread_copy(r_bc, ("r", 1))
-                w_transpose(2)
-                w_transpose(3)
-                spread_mm(wt, ("w", 1))
-                spread_copy(wt_bc, ("w", 1))
-                w_scale_out(2)
-                w_scale_out(3)
-                w_quantise(1)
-            elif kind == "SAN":
-                sanitise_masks(n)
-                sanitise_apply(n)
-                st["san"] = n
-                san_step[n] = st["step"]
+        def pull():
+            kind, n, m = queue[state["next"]]
+            state["next"] += 1
+            if kind == "w_side":
+                w_side(n)
+            elif kind == "sanitise":
+                sanitise_factor(n, m)
+                sanitise_apply(n, m)
+                state["sanitised"] = m - 1
+                for g in range(n, m):
+                    sanitise_step[g] = state["step"]
             else:
                 g = group_of(n)
-                while st["te"] < g:
-                    do_te(st["te"] + 1)
-                while st["q"] < g:
-                    do_q(st["q"] + 1)
-                if not st["ts"] and any(i >= 8 for (i, h) in units[n]):
-                    time_coordinate(1, 4)
-                    st["ts"] = True
-                mm(n)
-                a_c(n)
-                ac_done.add(n)
+                while state["turned"] < g:
+                    turn(state["turned"] + 1)
+                while state["quantised"] < g:
+                    quantise(state["quantised"] + 1)
+                if not state["late_t"] and any(i >= CHUNK for (i, h) in units[n]):
+                    time_coordinates(1, TILES // CHUNK)
+                    state["late_t"] = True
+                dot(n)
+                make_x(n)
+                x_made.add(n)
 
         def pull_until(u):
-            while u not in ac_done:
-                pull_one()
+            while u not in x_made:
+                pull()
 
-        def flush():
-            st["step"] += 1
-            while st["q"] < st["te"] and te_step[st["q"] + 1] + Q_LAG <= st["step"]:
-                do_q(st["q"] + 1)
-            while st["te"] < st["san"] and san_step[st["te"] + 1] + TE_LAG <= st["step"]:
-                do_te(st["te"] + 1)
+        def advance():
+            state["step"] += 1
+            while state["quantised"] < state["turned"] and turn_step[state["quantised"] + 1] + QUANTISE_LAG <= state["step"]:
+                quantise(state["quantised"] + 1)
+            while state["turned"] < state["sanitised"] and sanitise_step[state["turned"] + 1] + TRANSPOSE_LAG <= state["step"]:
+                turn(state["turned"] + 1)
 
-        for k in range(K0):
-            pull_one()
-        u0 = 0
-        for nb in BATCHES:
-            for u in range(u0, u0 + nb):
+        for k in range(FIRST_PULLS):
+            pull()
+        batch_start = 0
+        for size in BATCHES:
+            for u in range(batch_start, batch_start + size):
                 pull_until(u)
-                flush()
-                sq(u)
-                pull_until(min(n_units - 1, u + LA))
-                zz(u)
-            for u in range(u0, u0 + nb):
-                flush()
-                ln(u)
-                fin(u)
-            u0 += nb
+                advance()
+                roots(u)
+                pull_until(min(n_units - 1, u + LOOKAHEAD))
+                add_roots(u)
+            for u in range(batch_start, batch_start + size):
+                advance()
+                logarithm(u)
+                finish(u)
+            batch_start += size

@@ -34,7 +34,7 @@ A_TILES = 9
 SANITISE_LEAD = 4
 TRANSPOSE_LAG = 2
 QUANTISE_LAG = 1
-SCALAR_CLIPS = 7
+SCALAR_CLIPS = 10
 FIRST_PULLS = 3
 
 

from contextlib import ExitStack

import concourse.mybir as mybir
from concourse.masks import make_identity

F32 = mybir.dt.float32
BF16 = mybir.dt.bfloat16
U32 = mybir.dt.uint32
U8 = mybir.dt.uint8
FP8X4 = mybir.dt.float8_e4m3fn_x4
ALU = mybir.AluOpType
ACT = mybir.ActivationFunctionType

P = 128
TOKENS = 4096
VOCAB = 1024
K = 512
BANK = 512
TILES = TOKENS // P
CHUNK = 8
GROUP = 4
GROUPS = TILES // GROUP
W_TILES = VOCAB // P
SLOT = 528
FMAX = 3.3895313892515355e38
C_INF = 1.0e4 / FMAX
SUMSQ_MAX = 7.0e3
FLOPS = 2 * TOKENS * VOCAB * K

BATCHES = (10, 10)
LOOKAHEAD = 4
X_TILES = 5
A_TILES = 9
SANITISE_LEAD = 4
TRANSPOSE_LAG = 2
QUANTISE_LAG = 1
SCALAR_CLIPS = 10
FIRST_PULLS = 3


def make_units():
    units = [[(0, 0)], [(1, 0)], [(2, 0), (3, 0)], [(i, 1) for i in range(GROUP)]]
    place = [(0, 0), (0, 1), (0, 2), (1, 0)]
    for i in range(GROUP, TILES - 2, 2):
        place.append((len(units) - 2, 0))
        units.append([(i, 0), (i, 1), (i + 1, 0), (i + 1, 1)])
    last = len(units) - 2
    units.extend([[(TILES - 2, 0), (TILES - 2, 1)], [(TILES - 1, 0)], [(TILES - 1, 1)]])
    place.extend([(last, 0), (last, 2), (last, 3)])
    return units, place


def tile_geodesiclmheadv2_t_kernel(tc, hidden_states, weight, logit_scale, out):
    nc = tc.nc
    hid = hidden_states.flatten_outer_dims().rearrange("(p i) c -> p i c", i=TILES)
    out_tiles = out.flatten_outer_dims().rearrange("(p i) v -> p i v", i=TILES)
    out_flat = out.flatten_outer_dims().rearrange("(p i) v -> p (i v)", i=TILES)
    w_rows = weight.rearrange("(j p) k -> p j k", p=P)
    units, place = make_units()
    n_units = len(units)

    with ExitStack() as ctx:
        keep = ctx.enter_context(tc.tile_pool(name="keep", bufs=1))
        grouped_pool = ctx.enter_context(tc.tile_pool(name="grouped", bufs=3))
        x_pool = ctx.enter_context(tc.tile_pool(name="x", bufs=X_TILES))
        a_pool = ctx.enter_context(tc.tile_pool(name="a", bufs=A_TILES))
        turn_pool = ctx.enter_context(tc.psum_pool(name="turn", bufs=4))
        sum_pool = ctx.enter_context(tc.psum_pool(name="sum", bufs=4))
        ctx.enter_context(tc.manual_schedule())

        ident = keep.tile([P, P], F32, name="ident")
        one = keep.tile([P, 1], F32, name="one")
        minus_one = keep.tile([P, 1], F32, name="minus_one")
        floor_b = keep.tile([P, 1], F32, name="floor_b")
        scratch = keep.tile([P, 1], F32, name="scratch")
        ident_bf = keep.tile([P, P], BF16, name="ident_bf")
        make_identity(nc, ident[:])
        make_identity(nc, ident_bf[:])
        nc.vector.memset(one[:], 1.0)
        nc.vector.memset(minus_one[:], -1.0)
        nc.vector.memset(floor_b[:], 0.5e-12)
        nc.scalar.activation(out=scratch[:], in_=one[:], func=ACT.Sqrt)

        w_raw = [keep.tile([P, 2 * K], BF16, name="w_raw%d" % q) for q in range(W_TILES // 2)]
        for q in range(W_TILES // 2):
            nc.sync.dma_start(
                out=w_raw[q][:].rearrange("p (j k) -> p j k", k=K), in_=w_rows[:, 2 * q : 2 * q + 2, :]
            )
        h_raw = [keep.tile([P, CHUNK * SLOT], BF16, name="h_raw%d" % c) for c in range(TILES // CHUNK)]
        scale_raw = keep.tile([P, 1], BF16, name="scale_raw")
        for c in range(TILES // CHUNK):
            nc.sync.dma_start(
                out=h_raw[c][:].rearrange("p (i c) -> p i c", c=SLOT)[:, :, 1 : K + 2],
                in_=hid[:, CHUNK * c : CHUNK * (c + 1), :],
            )
            if c == 0:
                nc.sync.dma_start(out=scale_raw[:], in_=logit_scale.partition_broadcast(P))

        def nan_to_num_factor(eng, up, down, x):
            eng.tensor_scalar(out=up, in0=x, scalar1=FMAX, scalar2=C_INF, op0=ALU.is_le, op1=ALU.add)
            eng.tensor_scalar(out=down, in0=x, scalar1=-FMAX, scalar2=C_INF, op0=ALU.is_ge, op1=ALU.add)

        t_raw = keep.tile([P, TILES], F32, name="t_raw")
        t_up = keep.tile([P, TILES], F32, name="t_up")
        t_down = keep.tile([P, TILES], F32, name="t_down")
        t_coord = keep.tile([P, TILES], F32, name="t_coord")

        def time_coordinates(c0, c1):
            for c in range(c0, c1):
                nc.gpsimd.tensor_copy(
                    out=t_raw[:, CHUNK * c : CHUNK * (c + 1)].unsqueeze(2),
                    in_=h_raw[c][:].rearrange("p (i c) -> p i c", c=SLOT)[:, :, 1:2],
                )
            s = slice(CHUNK * c0, CHUNK * c1)
            nan_to_num_factor(nc.gpsimd, t_up[:, s], t_down[:, s], t_raw[:, s])
            nc.gpsimd.tensor_tensor(out=t_up[:, s], in0=t_up[:, s], in1=t_down[:, s], op=ALU.mult)
            nc.gpsimd.tensor_scalar(
                out=t_raw[:, s], in0=t_raw[:, s], scalar1=-FMAX, scalar2=FMAX, op0=ALU.max, op1=ALU.min
            )
            nc.gpsimd.tensor_tensor(out=t_coord[:, s], in0=t_raw[:, s], in1=t_up[:, s], op=ALU.mult)

        time_coordinates(0, 1)
        tau = keep.tile([P, 1], F32, name="tau")
        not_neg = keep.tile([P, 1], F32, name="not_neg")
        neg = keep.tile([P, 1], F32, name="neg")
        minus_4tau = keep.tile([P, 1], F32, name="minus_4tau")
        nc.gpsimd.tensor_scalar(out=tau[:], in0=scale_raw[:], scalar1=0.01, scalar2=2.5, op0=ALU.max, op1=ALU.min)
        nc.gpsimd.tensor_scalar(out=not_neg[:], in0=scale_raw[:], scalar1=0.0, scalar2=-4.0, op0=ALU.is_ge, op1=ALU.mult)
        nc.gpsimd.tensor_scalar(out=neg[:], in0=scale_raw[:], scalar1=0.0, scalar2=-4.0, op0=ALU.is_lt, op1=ALU.mult)
        nc.gpsimd.tensor_tensor(out=not_neg[:], in0=not_neg[:], in1=neg[:], op=ALU.add)
        nc.gpsimd.tensor_tensor(out=minus_4tau[:], in0=tau[:], in1=not_neg[:], op=ALU.mult)

        h_codes = [keep.tile([P, GROUP * P], U32, name="h_codes%d" % g, align_bytes=64) for g in range(GROUPS)]
        h_scales = [keep.tile([P, GROUP * P], U8, name="h_scales%d" % g, align_bytes=64) for g in range(GROUPS)]
        factor_up = keep.tile([P, CHUNK * K], BF16, name="factor_up")
        factor_down = keep.tile([P, CHUNK * K], BF16, name="factor_down")
        grouped_of = {}
        turned_of = {}

        def sanitise_factor(g0, g1):
            n = (g1 - g0) * GROUP
            first = (g0 % 2) * GROUP
            x = h_raw[g0 // 2][:].rearrange("p (i c) -> p i c", c=SLOT)[:, first : first + n, 2 : K + 2]
            up = factor_up[:, 0 : n * K].rearrange("p (i c) -> p i c", c=K)
            down = factor_down[:, 0 : n * K].rearrange("p (i c) -> p i c", c=K)
            nan_to_num_factor(nc.vector, up, down, x)

        def sanitise_apply(g0, g1):
            n = (g1 - g0) * GROUP
            first = (g0 % 2) * GROUP
            x = h_raw[g0 // 2][:].rearrange("p (i c) -> p i c", c=SLOT)[:, first : first + n, 2 : K + 2]
            nc.vector.tensor_tensor(
                out=factor_up[:, 0 : n * K], in0=factor_up[:, 0 : n * K], in1=factor_down[:, 0 : n * K], op=ALU.mult
            )
            nc.vector.tensor_scalar(out=x, in0=x, scalar1=-FMAX, scalar2=FMAX, op0=ALU.max, op1=ALU.min)
            nc.vector.tensor_tensor(
                out=x, in0=x, in1=factor_up[:, 0 : n * K].rearrange("p (i c) -> p i c", c=K), op=ALU.mult
            )

        def h_transpose(g):
            for pair in range(2):
                turned = turn_pool.tile([P, BANK], F32, name="turned", tag="turn")
                turned_of[(g, pair)] = turned
                for ii in range(2):
                    i = GROUP * g + 2 * pair + ii
                    words = h_raw[i // CHUNK][:].bitcast(F32)
                    base = (i % CHUNK) * (SLOT // 2) + 1
                    for u in range(2):
                        nc.tensor.transpose(
                            out=turned[:, u * 2 * P + ii * P : u * 2 * P + (ii + 1) * P],
                            in_=words[:, base + u * P : base + (u + 1) * P],
                            identity=ident[:],
                        )

        def h_copy_out(g):
            grouped_of[g] = grouped_pool.tile([P, GROUP * K], BF16, name="grouped", tag="grouped", align_bytes=64)
            words = grouped_of[g][:].bitcast(F32).rearrange("p (t u) -> p t u", u=2)
            for pair in range(2):
                nc.scalar.copy(
                    out=words[:, pair * 2 * P : (pair + 1) * 2 * P, :],
                    in_=turned_of[(g, pair)][:].rearrange("p (u t) -> p t u", u=2),
                )

        def h_quantise(g):
            nc.vector.quantize_mx(out=h_codes[g][:].bitcast(FP8X4), scales=h_scales[g][:], in_=grouped_of[g][:])

        sumsq_s = keep.tile([P, W_TILES], F32, name="sumsq_s")
        sumsq = keep.tile([P, W_TILES], F32, name="sumsq")
        squares_s = keep.tile([P, K], BF16, name="squares_s")
        squares_v = keep.tile([P, K], F32, name="squares_v")

        def w_row_tile(j):
            return w_raw[j // 2][:, (j % 2) * K : (j % 2 + 1) * K]

        for j in (0, 1, 4, 5):
            nc.scalar.activation(out=squares_s[:], in_=w_row_tile(j), func=ACT.Square, accum_out=sumsq_s[:, j : j + 1])
        for j in (2, 3, 6, 7):
            nc.vector.scalar_tensor_tensor(
                out=squares_v[:], in0=w_row_tile(j), scalar=1.0, in1=w_row_tile(j), op0=ALU.mult, op1=ALU.mult,
                accum_out=sumsq[:, j : j + 1],
            )
        nc.vector.tensor_copy(
            out=sumsq[:].rearrange("p (a b) -> p a b", b=4)[:, :, 0:2],
            in_=sumsq_s[:].rearrange("p (a b) -> p a b", b=4)[:, :, 0:2],
        )
        row_ok = keep.tile([P, W_TILES], F32, name="row_ok")
        nc.vector.tensor_single_scalar(out=row_ok[:], in_=sumsq[:], scalar=FMAX, op=ALU.is_le)
        nc.vector.tensor_scalar(out=sumsq[:], in0=sumsq[:], scalar1=1.0e-30, scalar2=SUMSQ_MAX, op0=ALU.max, op1=ALU.min)

        norm = keep.tile([P, W_TILES], F32, name="norm")
        e_plus = keep.tile([P, W_TILES], F32, name="e_plus")
        e_minus = keep.tile([P, W_TILES], F32, name="e_minus")
        nc.scalar.activation(out=norm[:], in_=sumsq[:], func=ACT.Sqrt)
        nc.scalar.activation(out=e_plus[:], in_=norm[:], func=ACT.Exp)
        nc.scalar.activation(out=e_minus[:], in_=norm[:], func=ACT.Exp, scale=-1.0)
        nc.scalar.activation(out=scratch[:], in_=one[:], func=ACT.Sqrt)

        floor_n = keep.tile([P, W_TILES], F32, name="floor_n")
        slope = keep.tile([P, W_TILES], F32, name="slope")
        offset = keep.tile([P, W_TILES], F32, name="offset")
        large = keep.tile([P, W_TILES], F32, name="large")
        diff = keep.tile([P, W_TILES], F32, name="diff")
        total = keep.tile([P, W_TILES], F32, name="total")
        r_col = keep.tile([P, W_TILES], F32, name="r_col")
        cosh_col = keep.tile([P, W_TILES], F32, name="cosh_col")
        nc.vector.tensor_scalar_max(out=floor_n[:], in0=norm[:], scalar1=1.0e-7)
        nc.vector.reciprocal(out=slope[:], in_=floor_n[:])
        nc.vector.tensor_single_scalar(out=large[:], in_=norm[:], scalar=1.0e-7, op=ALU.is_gt)
        nc.vector.scalar_tensor_tensor(out=slope[:], in0=slope[:], scalar=0.5, in1=large[:], op0=ALU.mult, op1=ALU.mult)
        nc.vector.tensor_tensor(out=slope[:], in0=slope[:], in1=row_ok[:], op=ALU.mult)
        nc.vector.scalar_tensor_tensor(out=offset[:], in0=large[:], scalar=-1.0, in1=row_ok[:], op0=ALU.mult, op1=ALU.add)
        nc.vector.tensor_scalar_max(out=offset[:], in0=offset[:], scalar1=0.0)
        for q in range(W_TILES // 2):
            nc.vector.tensor_scalar(out=w_raw[q][:], in0=w_raw[q][:], scalar1=-FMAX, scalar2=FMAX, op0=ALU.max, op1=ALU.min)

        sanitise_factor(0, 1)
        nc.vector.tensor_tensor(out=diff[:], in0=e_plus[:], in1=e_minus[:], op=ALU.subtract)
        nc.vector.tensor_tensor(out=diff[:], in0=diff[:], in1=slope[:], op=ALU.mult)
        nc.vector.tensor_tensor(out=r_col[:], in0=diff[:], in1=offset[:], op=ALU.add)
        sanitise_apply(0, 1)
        nc.vector.tensor_tensor(out=total[:], in0=e_plus[:], in1=e_minus[:], op=ALU.add)
        nc.vector.scalar_tensor_tensor(out=cosh_col[:], in0=total[:], scalar=0.5, in1=row_ok[:], op0=ALU.mult, op1=ALU.mult)

        cosh_row = keep.tile([P, VOCAB], F32, name="cosh_row")
        spread_of = {}

        def spread(column, key):
            h = key[1]
            bank = sum_pool.tile([P, BANK], F32, name="spread", tag="sum")
            spread_of[key] = bank
            for jj in range(4):
                j = 4 * h + jj
                nc.tensor.matmul(
                    out=bank[:, jj * P : (jj + 1) * P],
                    lhsT=column[:, j : j + 1].to_broadcast([P, P]),
                    rhs=ident[:],
                    start=True,
                    stop=True,
                )

        def spread_copy(row, key):
            h = key[1]
            nc.scalar.copy(out=row[:, h * BANK : (h + 1) * BANK], in_=spread_of[key][:])

        w_space = keep.tile([P, W_TILES * K], BF16, name="w_space")
        w_grouped = [keep.tile([P, 4 * BANK], BF16, name="w_grouped%d" % h, align_bytes=64) for h in range(2)]
        w_codes = keep.tile([P, VOCAB], U32, name="w_codes", align_bytes=64)
        w_scales = keep.tile([P, VOCAB], U8, name="w_scales", align_bytes=64)
        w_turned = {}

        def w_scale(j):
            nc.scalar.activation(
                out=w_space[:, j * K : (j + 1) * K].rearrange("p (u e q) -> p u e q", u=2, e=2),
                in_=w_row_tile(j).rearrange("p (u q e) -> p u e q", u=2, e=2),
                func=ACT.Copy,
                scale=r_col[:, j : j + 1],
            )

        def w_transpose(q):
            turned = turn_pool.tile([P, 2 * BANK], BF16, name="w_turned", tag="turn")
            w_turned[q] = turned
            for jj in range(2):
                for t in range(4):
                    nc.tensor.transpose(
                        out=turned[:, (jj * 4 + t) * P : (jj * 4 + t + 1) * P],
                        in_=w_space[:, (2 * q + jj) * K + t * P : (2 * q + jj) * K + (t + 1) * P],
                        identity=ident_bf[:],
                    )

        def w_copy_out(q):
            nc.scalar.copy(
                out=w_grouped[q // 2][:, (q % 2) * 2 * BANK : (q % 2 + 1) * 2 * BANK].rearrange(
                    "p (j v t) -> p j v t", j=2, t=4
                ),
                in_=w_turned[q][:].rearrange("p (j t v) -> p j v t", j=2, t=4),
            )

        def w_quantise(h):
            nc.vector.quantize_mx(
                out=w_codes[:, h * BANK : (h + 1) * BANK].bitcast(FP8X4),
                scales=w_scales[:, h * BANK : (h + 1) * BANK],
                in_=w_grouped[h][:],
            )

        def w_side(h):
            for j in range(4 * h, 4 * h + 4):
                w_scale(j)
            w_transpose(2 * h)
            w_transpose(2 * h + 1)
            if h == 0:
                h_transpose(0)
            spread(cosh_col, ("cosh", h))
            w_copy_out(2 * h)
            w_copy_out(2 * h + 1)
            if h == 0:
                h_copy_out(0)
            spread_copy(cosh_row, ("cosh", h))
            w_quantise(h)

        w_side(0)
        h_quantise(0)

        dot_of = {}
        x_of = {}
        a_of = {}

        def columns(u):
            first = place[u][1] * BANK
            return slice(first, first + len(units[u]) * BANK)

        def dot(u):
            for k, (i, h) in enumerate(units[u]):
                g = i // GROUP
                tokens = slice((i % GROUP) * P, (i % GROUP + 1) * P)
                bank = sum_pool.tile([P, BANK], F32, name="dot", tag="sum")
                dot_of[(u, k)] = bank
                nc.tensor.matmul_mx(
                    out=bank[:],
                    lhsT=h_codes[g][:, tokens].bitcast(FP8X4),
                    lhsT_scale=h_scales[g][:, tokens],
                    rhs=w_codes[:, h * BANK : (h + 1) * BANK].bitcast(FP8X4),
                    rhs_scale=w_scales[:, h * BANK : (h + 1) * BANK],
                    start=True,
                    stop=True,
                )

        def make_x(u):
            tile_no, first = place[u]
            if tile_no not in x_of:
                x_of[tile_no] = x_pool.tile([P, 4 * BANK], F32, name="x", tag="x")
            x = x_of[tile_no]
            for k, (i, h) in enumerate(units[u]):
                nc.vector.scalar_tensor_tensor(
                    out=x[:, (first + k) * BANK : (first + k + 1) * BANK],
                    in0=cosh_row[:, h * BANK : (h + 1) * BANK],
                    scalar=t_coord[:, i : i + 1],
                    in1=dot_of[(u, k)][:],
                    op0=ALU.mult,
                    op1=ALU.subtract,
                )
            if u >= SCALAR_CLIPS:
                c = columns(u)
                nc.vector.tensor_scalar(out=x[:, c], in0=x[:, c], scalar1=-1.0, scalar2=0.0, op0=ALU.add, op1=ALU.max)

        def roots(u):
            tile_no = place[u][0]
            if tile_no not in a_of:
                a_of[tile_no] = a_pool.tile([P, 4 * BANK], F32, name="a", tag="a")
            a = a_of[tile_no]
            x = x_of[tile_no]
            c = columns(u)
            if u < SCALAR_CLIPS:
                nc.scalar.activation(out=x[:, c], in_=x[:, c], func=ACT.Relu, bias=minus_one[:, 0:1])
            nc.scalar.activation(out=a[:, c], in_=x[:, c], func=ACT.Sqrt, bias=one[:, 0:1], scale=0.5)
            nc.scalar.activation(out=x[:, c], in_=x[:, c], func=ACT.Sqrt, bias=floor_b[:, 0:1], scale=0.5)

        def add_roots(u):
            tile_no = place[u][0]
            c = columns(u)
            nc.vector.tensor_tensor(out=a_of[tile_no][:, c], in0=a_of[tile_no][:, c], in1=x_of[tile_no][:, c], op=ALU.add)

        def logarithm(u):
            a = a_of[place[u][0]]
            c = columns(u)
            nc.scalar.activation(out=a[:, c], in_=a[:, c], func=ACT.Ln)

        def finish(u):
            a = a_of[place[u][0]]
            c = columns(u)
            nc.vector.scalar_tensor_tensor(
                out=a[:, c], in0=a[:, c], scalar=minus_4tau[:, 0:1], in1=a[:, c], op0=ALU.mult, op1=ALU.mult
            )
            banks = units[u]
            i0, h0 = banks[0]
            if len(banks) > 1 and all(h == h0 for (i, h) in banks):
                nc.sync.dma_start(
                    out=out_tiles[:, i0 : i0 + len(banks), h0 * BANK : (h0 + 1) * BANK],
                    in_=a[:, c].rearrange("p (i c) -> p i c", c=BANK),
                )
            else:
                start = i0 * VOCAB + h0 * BANK
                nc.sync.dma_start(out=out_flat[:, start : start + len(banks) * BANK], in_=a[:, c])

        def group_of(u):
            return max(i // GROUP for (i, h) in units[u])

        queue = []
        sanitised = 0
        second_side = False
        for u in range(n_units):
            if not second_side and any(h == 1 for (i, h) in units[u]):
                queue.append(("w_side", 1, 1))
                second_side = True
            if sanitised < group_of(u):
                upto = sanitised + 1 if sanitised == 0 else sanitised + 2
                queue.append(("sanitise", sanitised + 1, upto + 1))
                sanitised = upto
            queue.append(("x", u, u))
        for r in range(SANITISE_LEAD):
            k = 1
            while k < len(queue):
                if queue[k][0] == "sanitise" and queue[k - 1][0] != "sanitise":
                    queue[k - 1], queue[k] = queue[k], queue[k - 1]
                    k += 1
                k += 1

        state = {"sanitised": 0, "turned": 0, "quantised": 0, "step": 0, "late_t": False, "next": 0}
        sanitise_step = {}
        turn_step = {}
        x_made = set()

        def turn(g):
            h_transpose(g)
            h_copy_out(g)
            state["turned"] = g
            turn_step[g] = state["step"]

        def quantise(g):
            h_quantise(g)
            state["quantised"] = g

        def pull():
            kind, n, m = queue[state["next"]]
            state["next"] += 1
            if kind == "w_side":
                w_side(n)
            elif kind == "sanitise":
                sanitise_factor(n, m)
                sanitise_apply(n, m)
                state["sanitised"] = m - 1
                for g in range(n, m):
                    sanitise_step[g] = state["step"]
            else:
                g = group_of(n)
                while state["turned"] < g:
                    turn(state["turned"] + 1)
                while state["quantised"] < g:
                    quantise(state["quantised"] + 1)
                if not state["late_t"] and any(i >= CHUNK for (i, h) in units[n]):
                    time_coordinates(1, TILES // CHUNK)
                    state["late_t"] = True
                dot(n)
                make_x(n)
                x_made.add(n)

        def pull_until(u):
            while u not in x_made:
                pull()

        def advance():
            state["step"] += 1
            while state["quantised"] < state["turned"] and turn_step[state["quantised"] + 1] + QUANTISE_LAG <= state["step"]:
                quantise(state["quantised"] + 1)
            while state["turned"] < state["sanitised"] and sanitise_step[state["turned"] + 1] + TRANSPOSE_LAG <= state["step"]:
                turn(state["turned"] + 1)

        for k in range(FIRST_PULLS):
            pull()
        batch_start = 0
        for size in BATCHES:
            for u in range(batch_start, batch_start + size):
                pull_until(u)
                advance()
                roots(u)
                pull_until(min(n_units - 1, u + LOOKAHEAD))
                add_roots(u)
            for u in range(batch_start, batch_start + size):
                advance()
                logarithm(u)
                finish(u)
            batch_start += size
